import numpy as np
import ml_dtypes


def mxq(x, axis, fmt="e4m3"):
    dtype, down = {"e4m3": (ml_dtypes.float8_e4m3fn, 7), "e5m2": (ml_dtypes.float8_e5m2, 14)}[fmt]
    v = np.moveaxis(np.asarray(x, np.float32).astype(ml_dtypes.bfloat16).astype(np.float64), axis, -1)
    blocks = v.reshape(v.shape[:-1] + (-1, 32))
    amax = np.abs(blocks).max(-1, keepdims=True)
    byte = np.maximum(np.where(amax > 0, np.frexp(amax)[1] - 1 + 127, 0) - down, 1)
    scale = np.exp2(byte - 127.0)
    codes = (blocks / scale).astype(np.float32).astype(dtype).astype(np.float64)
    return np.moveaxis((codes * scale).reshape(v.shape), -1, axis)


WIDE = False


def mx_kscale(k):
    if not WIDE:
        return np.ones(k)
    levels = np.array([10, -10, 5, -5, 0])
    if k % 512:
        return np.exp2(np.random.permutation(np.resize(levels, k // 32))).repeat(32)
    a = np.empty((k // 512, 16))
    for p in range(k // 512):
        a[p, :8] = np.random.permutation(np.resize(levels, 8))
        for g in range(8):
            far = levels[np.abs(levels - a[p, g]) >= 10]
            a[p, g + 8] = far[np.random.randint(len(far))]
    return np.exp2(a.ravel()).repeat(32)


BF16 = ml_dtypes.bfloat16


def bf(x):
    return np.asarray(x, np.float32).astype(BF16)


def f64(x):
    return np.asarray(x).astype(np.float64)


B, S, M, H, HKV, DH, R_T, R_H, R_W = 1, 1024, 1536, 12, 2, 128, 16, 24, 24
SECT = (2 * R_T, 2 * R_H, 2 * R_W)
NC = len(SECT)


def rotate_half(x):
    h = x.shape[-1] // 2
    return np.concatenate((-x[..., h:], x[..., :h]), axis=-1)


def mrope_combine(t):
    parts, off = [], 0
    for i, sz in enumerate(SECT):
        parts.append(t[i % NC, :, :, off:off + sz])
        off += sz
    return np.concatenate(parts, axis=-1)


def setup_inputs():
    s = mx_kscale(M)
    sd = 1.0 / np.sqrt(M)
    return {"hidden_states": bf(np.random.standard_normal((B, S, M)) * s),
            "cos": bf(np.random.standard_normal((NC, B, S, DH))),
            "sin": bf(np.random.standard_normal((NC, B, S, DH))),
            "Wq": bf(np.random.standard_normal((M, H, DH)) * sd / s[:, None, None]),
            "bq": bf(np.random.standard_normal((H, DH)) * 0.3),
            "Wk": bf(np.random.standard_normal((M, HKV, DH)) * sd / s[:, None, None]),
            "bk": bf(np.random.standard_normal((HKV, DH)) * 0.3),
            "Wv": bf(np.random.standard_normal((M, HKV, DH)) * sd / s[:, None, None]),
            "bv": bf(np.random.standard_normal((HKV, DH)) * 0.3)}


def reference(hidden_states, cos, sin, Wq, bq, Wk, bk, Wv, bv):
    xq = mxq(f64(hidden_states), 2, "e4m3")
    q = (xq @ mxq(f64(Wq).reshape(M, H * DH), 0, "e4m3")).reshape(B, S, H, DH) + f64(bq)
    k = (xq @ mxq(f64(Wk).reshape(M, HKV * DH), 0, "e4m3")).reshape(B, S, HKV, DH) + f64(bk)
    v = (xq @ mxq(f64(Wv).reshape(M, HKV * DH), 0, "e4m3")).reshape(B, S, HKV, DH) + f64(bv)
    cos_c = mrope_combine(f64(cos))[:, :, None, :]
    sin_c = mrope_combine(f64(sin))[:, :, None, :]
    q_rot = q * cos_c + rotate_half(q) * sin_c
    k_rot = k * cos_c + rotate_half(k) * sin_c
    return q_rot, k_rot, v

@@ -1,0 +1,310 @@
+from contextlib import ExitStack
+
+import concourse.mybir as mybir
+from concourse.masks import make_identity
+
+F32 = mybir.dt.float32
+BF16 = mybir.dt.bfloat16
+U32 = mybir.dt.uint32
+U8 = mybir.dt.uint8
+FP8X4 = mybir.dt.float8_e4m3fn_x4
+ADD = mybir.AluOpType.add
+MULT = mybir.AluOpType.mult
+ACT = mybir.ActivationFunctionType
+
+P = 128
+S = 1024
+M = 1536
+PASSES = 3
+T8 = 8
+HALF = 512
+
+FLOPS = 2 * S * M * 2048
+BYTES = S * M * 2 + M * 2048 * 2 + 16 * 128 * 2 + 2 * S * 128 * 2 + S * 2048 * 4
+
+COS_PARTS = ((0, 0, 32, 0), (1, 32, 80, 32), (2, 80, 128, 80))
+SIN_PARTS = ((1, 64, 80, 0), (2, 80, 128, 16), (0, 0, 32, 64), (1, 32, 64, 96))
+
+
+def tile_qwen2vlattention_pa_kernel(
+    tc, hidden_states, cos, sin, Wq, bq, Wk, bk, Wv, bv, out_0, out_1, out_2
+):
+    nc = tc.nc
+    x_v = hidden_states.rearrange("b s m -> (b s) m").rearrange("(p t) m -> p t m", t=T8)
+    cos_v = cos.rearrange("c b s d -> c (b s) d")
+    sin_v = sin.rearrange("c b s d -> c (b s) d")
+    wq_v = Wq.rearrange("m h d -> m (h d)")
+    wk_v = Wk.rearrange("m h d -> m (h d)")
+    wv_v = Wv.rearrange("m h d -> m (h d)")
+    o0_v = out_0.rearrange("b s h d -> (b s) (h d)").rearrange("(p t) n -> p t n", t=T8)
+    o1_v = out_1.rearrange("b s h d -> (b s) (h d)").rearrange("(p t) n -> p t n", t=T8)
+    o2_v = out_2.rearrange("b s h d -> (b s) (h d)").rearrange("(p t) n -> p t n", t=T8)
+
+    with ExitStack() as ctx:
+        keep = ctx.enter_context(tc.tile_pool(name="keep", bufs=1))
+        xgp = ctx.enter_context(tc.tile_pool(name="xgp", bufs=3))
+        wgp = ctx.enter_context(tc.tile_pool(name="wgp", bufs=4))
+        uwp = ctx.enter_context(tc.tile_pool(name="uwp", bufs=2))
+        outp = ctx.enter_context(tc.tile_pool(name="outp", bufs=8))
+        psum = ctx.enter_context(tc.psum_pool(name="psum", bufs=1))
+        ctx.enter_context(tc.manual_schedule())
+
+        def bank(i, shape, dtype):
+            return psum.tile(shape, dtype, name="bank%d" % i, tag="bank%d" % i)
+
+        ident_f = keep.tile([P, P], F32, name="ident_f")
+        ident_b = keep.tile([P, P], BF16, name="ident_b")
+        perm_f = keep.tile([P, P], F32, name="perm_f")
+        sgn = keep.tile([P, 1], F32, name="sgn")
+        b_raw = keep.tile([P, P], BF16, name="b_raw")
+        b_t = keep.tile([P, 16], F32, name="b_t")
+        c_raw = keep.tile([P, T8, P], BF16, name="c_raw")
+        s_raw = keep.tile([P, T8, P], BF16, name="s_raw")
+        tab_t = keep.tile([P, 2, 2, HALF], BF16, name="tab_t")
+        x_raw = keep.tile([P, T8 * M], BF16, name="x_raw")
+        xq = keep.tile([P, 2, PASSES, HALF], U32, name="xq", align_bytes=64)
+        xs = keep.tile([P, 2, PASSES, HALF], U8, name="xs", align_bytes=64)
+        wq = [keep.tile([P, PASSES, 512], U32, name="wq%d" % j, align_bytes=64) for j in range(4)]
+        ws = [keep.tile([P, PASSES, 512], U8, name="ws%d" % j, align_bytes=64) for j in range(4)]
+        w_raw = [
+            [keep.tile([P, 2, 4, 256], BF16, name="wraw%d_%d" % (j, g)) for g in range(PASSES)]
+            if j == 0
+            else [keep.tile([P, 1, 4, 512], BF16, name="wraw%d_%d" % (j, g)) for g in range(PASSES)]
+            for j in range(4)
+        ]
+        x_w = x_raw[:].bitcast(F32)
+
+        make_identity(nc, ident_f[:])
+        make_identity(nc, ident_b[:])
+        nc.vector.memset(b_raw[:], 0.0)
+        nc.vector.memset(sgn[0:64, :], 1.0)
+        nc.vector.memset(sgn[64:128, :], -1.0)
+        nc.vector.tensor_copy(out=perm_f[:, 0:64], in_=ident_f[:, 64:128])
+        nc.vector.tensor_copy(out=perm_f[:, 64:128], in_=ident_f[:, 0:64])
+
+        def load_x(half):
+            for tp in range(2):
+                t8 = 4 * half + 2 * tp
+                nc.sync.dma_start(
+                    out=x_raw[:, t8 * M : (t8 + 2) * M],
+                    in_=x_v[:, t8 : t8 + 2, :].rearrange("p t m -> p (t m)"),
+                )
+
+        def load_w(j):
+            for g in range(PASSES):
+                rows = slice(512 * g, 512 * g + 512)
+                if j == 0:
+                    sources = (wk_v[rows, :], wv_v[rows, :])
+                else:
+                    sources = (wq_v[rows, 512 * (j - 1) : 512 * j],)
+                for blk, src in enumerate(sources):
+                    nc.sync.dma_start(
+                        out=w_raw[j][g][:, blk],
+                        in_=src.rearrange("(q e) n -> q e n", e=4),
+                    )
+
+        def load_tables(half):
+            ts = slice(4 * half, 4 * half + 4)
+            for comp, lo, hi, dlo in COS_PARTS:
+                src = cos_v[comp].rearrange("(p t) d -> p t d", t=T8)
+                nc.sync.dma_start(out=c_raw[:, ts, dlo : dlo + hi - lo], in_=src[:, ts, lo:hi])
+            for comp, lo, hi, dlo in SIN_PARTS:
+                src = sin_v[comp].rearrange("(p t) d -> p t d", t=T8)
+                nc.sync.dma_start(out=s_raw[:, ts, dlo : dlo + hi - lo], in_=src[:, ts, lo:hi])
+
+        load_x(0)
+        load_w(0)
+        nc.sync.dma_start(out=b_raw[0:12, :], in_=bq)
+        nc.sync.dma_start(out=b_raw[12:14, :], in_=bk)
+        nc.sync.dma_start(out=b_raw[14:16, :], in_=bv)
+        load_tables(0)
+        load_tables(1)
+        load_x(1)
+        load_w(1)
+        load_w(2)
+        load_w(3)
+
+        xg = {}
+        wg = {}
+        accs = {}
+        uws = {}
+
+        def bias_column(j, hh):
+            return 12 + hh if j == 0 else 4 * (j - 1) + hh
+
+        def rotated(j, hh):
+            return j > 0 or hh < 2
+
+        def x_transposes(half, banks):
+            words = []
+            for g in range(PASSES):
+                grouped = xgp.tile([P, 2048], BF16, name="xg", tag="xg", align_bytes=64)
+                xg[(half, g)] = grouped
+                words.append(grouped[:].bitcast(F32).rearrange("p (tt s u) -> p tt s u", tt=4, u=2))
+            for tp in range(2):
+                for g in range(PASSES):
+                    xt = bank(banks[PASSES * tp + g], [P, 2, 2, P], F32)
+                    for tt in range(2):
+                        for u in range(2):
+                            col = (4 * half + 2 * tp + tt) * (M // 2) + 256 * g
+                            nc.tensor.transpose(xt[:, tt, u, :], x_w[:, col + u : col + 256 : 2], ident_f[:])
+                    nc.scalar.copy(
+                        out=words[g][:, 2 * tp : 2 * tp + 2],
+                        in_=xt[:].rearrange("p tt u s -> p tt s u"),
+                    )
+
+        def quant_x(half, g):
+            nc.vector.quantize_mx(
+                out=xq[:, half, g, :].bitcast(FP8X4), scales=xs[:, half, g, :], in_=xg[(half, g)][:]
+            )
+
+        def regroup(on_vector, j, g):
+            grouped = wgp.tile([P, 2048], BF16, name="wg", tag="wg", align_bytes=64)
+            wg[(j, g)] = grouped
+            blocks = w_raw[j][g].shape[1]
+            dst = grouped[:].rearrange("p (b c i t) -> p b c t i", b=blocks, i=4, t=4)
+            src = w_raw[j][g][:].rearrange("p b t (c i) -> p b c t i", i=4)
+            for blk in range(blocks):
+                if on_vector:
+                    nc.vector.tensor_copy(out=dst[:, blk], in_=src[:, blk])
+                else:
+                    nc.scalar.copy(out=dst[:, blk], in_=src[:, blk])
+
+        def quant_w(j, g):
+            nc.vector.quantize_mx(
+                out=wq[j][:, g, :].bitcast(FP8X4), scales=ws[j][:, g, :], in_=wg[(j, g)][:]
+            )
+
+        def project(r, banks, pass_outer):
+            j, half = divmod(r, 2)
+            tiles = [bank(b, [P, HALF], F32) for b in banks]
+            accs[r] = tiles
+            if pass_outer:
+                order = [(g, hh) for g in range(PASSES) for hh in range(4)]
+            else:
+                order = [(g, hh) for hh in range(4) for g in range(PASSES)]
+            for g, hh in order:
+                cols = slice(P * hh, P * hh + P)
+                nc.tensor.matmul_mx(
+                    out=tiles[hh][:],
+                    lhsT=wq[j][:, g, cols].bitcast(FP8X4),
+                    lhsT_scale=ws[j][:, g, cols],
+                    rhs=xq[:, half, g, :].bitcast(FP8X4),
+                    rhs_scale=xs[:, half, g, :],
+                    start=(g == 0),
+                    stop=(g == PASSES - 1),
+                )
+
+        def bias_transpose(b):
+            bt = bank(b, [P, P], BF16)
+            nc.tensor.transpose(bt[:], b_raw[:], ident_b[:])
+            nc.vector.tensor_copy(out=b_t[:], in_=bt[:, 0:16])
+
+        def table_transposes(half, b):
+            tb = bank(b, [P, 2, HALF], BF16)
+            for t in range(4):
+                nc.tensor.transpose(tb[:, 0, P * t : P * t + P], c_raw[:, 4 * half + t, :], ident_b[:])
+            for t in range(4):
+                nc.tensor.transpose(tb[:, 1, P * t : P * t + P], s_raw[:, 4 * half + t, :], ident_b[:])
+            nc.scalar.copy(out=tab_t[:, half, 0, :], in_=tb[:, 0, :])
+            nc.scalar.activation(out=tab_t[:, half, 1, :], in_=tb[:, 1, :], func=ACT.Copy, scale=sgn[:, 0:1])
+
+        def rope(r, extras):
+            j, half = divmod(r, 2)
+            uws[r] = []
+            for hh in range(4):
+                col = bias_column(j, hh)
+                acc = accs[r][hh]
+                uw = uwp.tile([P, 2, HALF], F32, name="uw%d" % hh, tag="uw%d" % hh)
+                uws[r].append(uw)
+                if rotated(j, hh):
+                    nc.vector.scalar_tensor_tensor(
+                        out=uw[:],
+                        in0=acc[:].unsqueeze(1).to_broadcast([P, 2, HALF]),
+                        scalar=b_t[:, col : col + 1],
+                        in1=tab_t[:, half],
+                        op0=ADD,
+                        op1=MULT,
+                    )
+                else:
+                    nc.scalar.activation(
+                        out=uw[:, 0, :], in_=acc[:], func=ACT.Identity, bias=b_t[:, col : col + 1]
+                    )
+                for extra in extras[hh]:
+                    extra()
+
+        def back(r):
+            j, half = divmod(r, 2)
+            for tp in range(2):
+                pair = (2 * tp, 2 * tp + 1)
+                o_ps = [bank(t, [P, 512], F32) for t in pair]
+                for hh in range(4):
+                    uw = uws[r][hh]
+                    cols = slice(P * hh, P * hh + P)
+                    if rotated(j, hh):
+                        for o_t, t in zip(o_ps, pair):
+                            nc.tensor.matmul(
+                                out=o_t[:, cols], lhsT=uw[:, 0, P * t : P * t + P], rhs=ident_f[:],
+                                is_transpose=True, start=True, stop=False,
+                            )
+                        for o_t, t in zip(o_ps, pair):
+                            nc.tensor.matmul(
+                                out=o_t[:, cols], lhsT=uw[:, 1, P * t : P * t + P], rhs=perm_f[:],
+                                is_transpose=True, start=False, stop=True,
+                            )
+                    else:
+                        for o_t, t in zip(o_ps, pair):
+                            nc.tensor.transpose(o_t[:, cols], uw[:, 0, P * t : P * t + P], ident_f[:])
+                for o_t, t in zip(o_ps, pair):
+                    o_sb = outp.tile([P, 512], F32, name="o_sb", tag="o_sb")
+                    nc.scalar.copy(out=o_sb[:], in_=o_t[:])
+                    t8 = 4 * half + t
+                    if j == 0:
+                        nc.sync.dma_start(out=o1_v[:, t8, :], in_=o_sb[:, 0:256])
+                        nc.sync.dma_start(out=o2_v[:, t8, :], in_=o_sb[:, 256:512])
+                    else:
+                        nc.sync.dma_start(out=o0_v[:, t8, 512 * (j - 1) : 512 * j], in_=o_sb[:])
+
+        x_transposes(0, (0, 1, 2, 3, 4, 5))
+        regroup(True, 0, 0)
+        quant_x(0, 0)
+        regroup(True, 0, 1)
+        quant_x(0, 1)
+        quant_w(0, 0)
+        regroup(True, 0, 2)
+        quant_x(0, 2)
+        quant_w(0, 1)
+        quant_w(0, 2)
+        project(0, (0, 1, 2, 3), True)
+        bias_transpose(6)
+        table_transposes(0, 7)
+        table_transposes(1, 6)
+        x_transposes(1, (4, 5, 7, 6, 4, 5))
+        rope(0, [[], [lambda: quant_x(1, 0)], [lambda: quant_x(1, 1)], [lambda: quant_x(1, 2)]])
+        project(1, (4, 5, 6, 7), False)
+
+        def passes_due(r):
+            if r == 0:
+                return [(1, 0), (1, 1), (1, 2)]
+            if r % 2 == 1 and (r + 3) // 2 < 4:
+                return [((r + 3) // 2, 0), ((r + 3) // 2, 1)]
+            if r % 2 == 0 and (r + 2) // 2 < 4:
+                return [((r + 2) // 2, 2)]
+            return []
+
+        def later(fn, j, g):
+            return lambda: fn(j, g)
+
+        for r in range(8):
+            extras = [[], [], [], []]
+            for k, (j, g) in enumerate(passes_due(r)):
+                if r == 0 and g == 1:
+                    extras[0].append(lambda: regroup(True, 1, 1))
+                else:
+                    regroup(False, j, g)
+                extras[k + 1].append(later(quant_w, j, g))
+            back(r)
+            if r + 1 < 8:
+                rope(r + 1, extras)
+            if r + 2 < 8:
+                project(r + 2, (4, 5, 6, 7), False)

@@ -9,6 +9,7 @@ U32 = mybir.dt.uint32
 U8 = mybir.dt.uint8
 FP8X4 = mybir.dt.float8_e4m3fn_x4
 ADD = mybir.AluOpType.add
+SUB = mybir.AluOpType.subtract
 MULT = mybir.AluOpType.mult
 ACT = mybir.ActivationFunctionType
 
@@ -42,10 +43,12 @@ def tile_qwen2vlattention_pa_kernel(
 
     with ExitStack() as ctx:
         keep = ctx.enter_context(tc.tile_pool(name="keep", bufs=1))
-        xgp = ctx.enter_context(tc.tile_pool(name="xgp", bufs=3))
+        xgp = ctx.enter_context(tc.tile_pool(name="xgp", bufs=4))
+        wrp = ctx.enter_context(tc.tile_pool(name="wrp", bufs=8))
         wgp = ctx.enter_context(tc.tile_pool(name="wgp", bufs=4))
         uwp = ctx.enter_context(tc.tile_pool(name="uwp", bufs=2))
-        outp = ctx.enter_context(tc.tile_pool(name="outp", bufs=8))
+        krp = ctx.enter_context(tc.tile_pool(name="krp", bufs=2))
+        outp = ctx.enter_context(tc.tile_pool(name="outp", bufs=6))
         psum = ctx.enter_context(tc.psum_pool(name="psum", bufs=1))
         ctx.enter_context(tc.manual_schedule())
 
@@ -55,9 +58,17 @@ def tile_qwen2vlattention_pa_kernel(
         ident_f = keep.tile([P, P], F32, name="ident_f")
         ident_b = keep.tile([P, P], BF16, name="ident_b")
         perm_f = keep.tile([P, P], F32, name="perm_f")
+        ones_b = keep.tile([P, P], BF16, name="ones_b")
         sgn = keep.tile([P, 1], F32, name="sgn")
+        warm = keep.tile([P, 1], F32, name="warm")
         b_raw = keep.tile([P, P], BF16, name="b_raw")
         b_t = keep.tile([P, 16], F32, name="b_t")
+        row_b = keep.tile([P, 768], BF16, name="row_b")
+        free_b = keep.tile([P, 768], F32, name="free_b")
+        qb_sb = keep.tile([P, T8, 256], F32, name="qb_sb")
+        kv_sb = keep.tile([P, T8, 512], F32, name="kv_sb")
+        c_all = keep.tile([P, 3, T8, P], BF16, name="c_all")
+        s_all = keep.tile([P, 3, T8, P], BF16, name="s_all")
         c_raw = keep.tile([P, T8, P], BF16, name="c_raw")
         s_raw = keep.tile([P, T8, P], BF16, name="s_raw")
         tab_t = keep.tile([P, 2, 2, HALF], BF16, name="tab_t")
@@ -67,18 +78,19 @@ def tile_qwen2vlattention_pa_kernel(
         wq = [keep.tile([P, PASSES, 512], U32, name="wq%d" % j, align_bytes=64) for j in range(4)]
         ws = [keep.tile([P, PASSES, 512], U8, name="ws%d" % j, align_bytes=64) for j in range(4)]
         w_raw = [
-            [keep.tile([P, 2, 4, 256], BF16, name="wraw%d_%d" % (j, g)) for g in range(PASSES)]
-            if j == 0
-            else [keep.tile([P, 1, 4, 512], BF16, name="wraw%d_%d" % (j, g)) for g in range(PASSES)]
+            [wrp.tile([P, 2, 4, 256] if j == 0 else [P, 1, 4, 512], BF16, name="wraw", tag="wraw") for g in range(PASSES)]
             for j in range(4)
         ]
         x_w = x_raw[:].bitcast(F32)
 
-        make_identity(nc, ident_f[:])
-        make_identity(nc, ident_b[:])
-        nc.vector.memset(b_raw[:], 0.0)
         nc.vector.memset(sgn[0:64, :], 1.0)
         nc.vector.memset(sgn[64:128, :], -1.0)
+        nc.scalar.copy(out=warm[:], in_=sgn[:])
+        make_identity(nc, ident_f[:])
+        make_identity(nc, ident_b[:])
+        nc.vector.memset(row_b[:], 0.0)
+        nc.vector.memset(b_raw[:], 0.0)
+        nc.vector.memset(ones_b[:], 1.0)
         nc.vector.tensor_copy(out=perm_f[:, 0:64], in_=ident_f[:, 64:128])
         nc.vector.tensor_copy(out=perm_f[:, 64:128], in_=ident_f[:, 0:64])
 
@@ -103,24 +115,19 @@ def tile_qwen2vlattention_pa_kernel(
                         in_=src.rearrange("(q e) n -> q e n", e=4),
                     )
 
-        def load_tables(half):
-            ts = slice(4 * half, 4 * half + 4)
-            for comp, lo, hi, dlo in COS_PARTS:
-                src = cos_v[comp].rearrange("(p t) d -> p t d", t=T8)
-                nc.sync.dma_start(out=c_raw[:, ts, dlo : dlo + hi - lo], in_=src[:, ts, lo:hi])
-            for comp, lo, hi, dlo in SIN_PARTS:
-                src = sin_v[comp].rearrange("(p t) d -> p t d", t=T8)
-                nc.sync.dma_start(out=s_raw[:, ts, dlo : dlo + hi - lo], in_=src[:, ts, lo:hi])
+        def load_tables():
+            for table, view in ((c_all, cos_v), (s_all, sin_v)):
+                nc.sync.dma_start(out=table[:], in_=view.rearrange("c (p t) d -> p c t d", t=T8))
 
         load_x(0)
+        nc.gpsimd.dma_start(out=row_b[0:1, 0:256], in_=bk.rearrange("(o h) d -> o (h d)", o=1))
+        nc.gpsimd.dma_start(out=row_b[0:1, 256:512], in_=bv.rearrange("(o h) d -> o (h d)", o=1))
+        nc.gpsimd.dma_start(out=row_b[0:1, 512:768], in_=bq[0:2, :].rearrange("(o h) d -> o (h d)", o=1))
+        nc.gpsimd.dma_start(out=b_raw[0:12, :], in_=bq)
         load_w(0)
-        nc.sync.dma_start(out=b_raw[0:12, :], in_=bq)
-        nc.sync.dma_start(out=b_raw[12:14, :], in_=bk)
-        nc.sync.dma_start(out=b_raw[14:16, :], in_=bv)
-        load_tables(0)
-        load_tables(1)
         load_x(1)
         load_w(1)
+        load_tables()
         load_w(2)
         load_w(3)
 
@@ -129,76 +136,153 @@ def tile_qwen2vlattention_pa_kernel(
         accs = {}
         uws = {}
 
-        def bias_column(j, hh):
-            return 12 + hh if j == 0 else 4 * (j - 1) + hh
+        def copy_on(engine, out, in_):
+            if engine == "v":
+                nc.vector.tensor_copy(out=out, in_=in_)
+            elif engine == "s":
+                nc.scalar.copy(out=out, in_=in_)
+            else:
+                nc.gpsimd.tensor_scalar(out=out, in0=in_, scalar1=1.0, scalar2=0.0, op0=MULT, op1=ADD)
 
-        def rotated(j, hh):
-            return j > 0 or hh < 2
-
-        def x_transposes(half, banks):
-            words = []
+        def x_transposes(half, tp, banks, engines):
             for g in range(PASSES):
-                grouped = xgp.tile([P, 2048], BF16, name="xg", tag="xg", align_bytes=64)
-                xg[(half, g)] = grouped
-                words.append(grouped[:].bitcast(F32).rearrange("p (tt s u) -> p tt s u", tt=4, u=2))
-            for tp in range(2):
-                for g in range(PASSES):
-                    xt = bank(banks[PASSES * tp + g], [P, 2, 2, P], F32)
-                    for tt in range(2):
-                        for u in range(2):
-                            col = (4 * half + 2 * tp + tt) * (M // 2) + 256 * g
-                            nc.tensor.transpose(xt[:, tt, u, :], x_w[:, col + u : col + 256 : 2], ident_f[:])
-                    nc.scalar.copy(
-                        out=words[g][:, 2 * tp : 2 * tp + 2],
-                        in_=xt[:].rearrange("p tt u s -> p tt s u"),
-                    )
+                if tp == 0:
+                    xg[(half, g)] = xgp.tile([P, 2048], BF16, name="xg", tag="xg", align_bytes=64)
+                words = xg[(half, g)][:].bitcast(F32).rearrange("p (tt s u) -> p tt s u", tt=4, u=2)
+                xt = bank(banks[g], [P, 2, 2, P], F32)
+                for tt in range(2):
+                    for u in range(2):
+                        col = (4 * half + 2 * tp + tt) * (M // 2) + 256 * g
+                        nc.tensor.transpose(xt[:, tt, u, :], x_w[:, col + u : col + 256 : 2], ident_f[:])
+                copy_on(engines[g], words[:, 2 * tp : 2 * tp + 2], xt[:].rearrange("p tt u s -> p tt s u"))
 
         def quant_x(half, g):
             nc.vector.quantize_mx(
                 out=xq[:, half, g, :].bitcast(FP8X4), scales=xs[:, half, g, :], in_=xg[(half, g)][:]
             )
 
-        def regroup(on_vector, j, g):
-            grouped = wgp.tile([P, 2048], BF16, name="wg", tag="wg", align_bytes=64)
-            wg[(j, g)] = grouped
-            blocks = w_raw[j][g].shape[1]
-            dst = grouped[:].rearrange("p (b c i t) -> p b c t i", b=blocks, i=4, t=4)
-            src = w_raw[j][g][:].rearrange("p b t (c i) -> p b c t i", i=4)
-            for blk in range(blocks):
-                if on_vector:
-                    nc.vector.tensor_copy(out=dst[:, blk], in_=src[:, blk])
-                else:
-                    nc.scalar.copy(out=dst[:, blk], in_=src[:, blk])
+        def regroup(engine, j, g, part):
+            if part == 0:
+                wg[(j, g)] = wgp.tile([P, 2048], BF16, name="wg", tag="wg", align_bytes=64)
+            dst = wg[(j, g)][:, 1024 * part : 1024 * part + 1024].rearrange("p (c i t) -> p c t i", i=4, t=4)
+            if j == 0:
+                src = w_raw[j][g][:, part]
+            else:
+                src = w_raw[j][g][:, 0, :, 256 * part : 256 * part + 256]
+            copy_on(engine, dst, src.rearrange("p t (c i) -> p c t i", i=4))
 
         def quant_w(j, g):
             nc.vector.quantize_mx(
                 out=wq[j][:, g, :].bitcast(FP8X4), scales=ws[j][:, g, :], in_=wg[(j, g)][:]
             )
 
-        def project(r, banks, pass_outer):
-            j, half = divmod(r, 2)
-            tiles = [bank(b, [P, HALF], F32) for b in banks]
-            accs[r] = tiles
-            if pass_outer:
-                order = [(g, hh) for g in range(PASSES) for hh in range(4)]
-            else:
-                order = [(g, hh) for hh in range(4) for g in range(PASSES)]
-            for g, hh in order:
-                cols = slice(P * hh, P * hh + P)
-                nc.tensor.matmul_mx(
-                    out=tiles[hh][:],
-                    lhsT=wq[j][:, g, cols].bitcast(FP8X4),
-                    lhsT_scale=ws[j][:, g, cols],
-                    rhs=xq[:, half, g, :].bitcast(FP8X4),
-                    rhs_scale=xs[:, half, g, :],
-                    start=(g == 0),
-                    stop=(g == PASSES - 1),
-                )
+        kv_acc = {}
+        qb_acc = {}
+
+        def kv_pass(half, g, t):
+            if g == 0:
+                kv_acc[(half, t)] = bank(4 * half + t, [P, 512], F32)
+            tok = slice(P * t, P * t + P)
+            nc.tensor.matmul_mx(
+                out=kv_acc[(half, t)][:],
+                lhsT=xq[:, half, g, tok].bitcast(FP8X4),
+                lhsT_scale=xs[:, half, g, tok],
+                rhs=wq[0][:, g, :].bitcast(FP8X4),
+                rhs_scale=ws[0][:, g, :],
+                start=(g == 0),
+                stop=(g == PASSES - 1),
+            )
+
+        def kv_add(half, t):
+            nc.vector.tensor_tensor(
+                out=kv_sb[:, 4 * half + t, :], in0=kv_acc[(half, t)][:], in1=free_b[:, 0:512], op=ADD
+            )
+
+        def qb_project(tp):
+            qb_acc[tp] = bank(4 + tp, [P, 2, 256], F32)
+            for tt in range(2):
+                half, t = divmod(2 * tp + tt, 4)
+                tok = slice(P * t, P * t + P)
+                for g in range(PASSES):
+                    nc.tensor.matmul_mx(
+                        out=qb_acc[tp][:, tt, :],
+                        lhsT=xq[:, half, g, tok].bitcast(FP8X4),
+                        lhsT_scale=xs[:, half, g, tok],
+                        rhs=wq[1][:, g, 0:256].bitcast(FP8X4),
+                        rhs_scale=ws[1][:, g, 0:256],
+                        start=(g == 0),
+                        stop=(g == PASSES - 1),
+                    )
+
+        def qb_add(tp):
+            nc.vector.tensor_tensor(
+                out=qb_sb[:, 2 * tp : 2 * tp + 2, :],
+                in0=qb_acc[tp][:],
+                in1=free_b[:, 512:768].unsqueeze(1).to_broadcast([P, 2, 256]),
+                op=ADD,
+            )
+
+        def v_store(half):
+            ts = slice(4 * half, 4 * half + 4)
+            nc.sync.dma_start(out=o2_v[:, ts, :], in_=kv_sb[:, ts, 256:512])
+
+        def free_rope(tile, tp):
+            ts = slice(2 * tp, 2 * tp + 2)
+            y = tile[:, ts, 0:256].rearrange("p t (h d) -> p t h d", h=2)
+            c_b = c_raw[:, ts, :].unsqueeze(2).to_broadcast([P, 2, 2, P])
+            s_b = s_raw[:, ts, :].unsqueeze(2).to_broadcast([P, 2, 2, P])
+            a = krp.tile([P, 2, 2, P], F32, name="ka", tag="ka")
+            w = krp.tile([P, 2, 2, P], F32, name="kw", tag="kw")
+            nc.gpsimd.tensor_tensor(out=a[:], in0=y, in1=c_b, op=MULT)
+            nc.gpsimd.tensor_tensor(out=w[:], in0=y, in1=s_b, op=MULT)
+            nc.gpsimd.tensor_tensor(out=y[:, :, :, 0:64], in0=a[:, :, :, 0:64], in1=w[:, :, :, 64:128], op=SUB)
+            nc.gpsimd.tensor_tensor(out=y[:, :, :, 64:128], in0=a[:, :, :, 64:128], in1=w[:, :, :, 0:64], op=ADD)
+
+        def k_store(half):
+            ts = slice(4 * half, 4 * half + 4)
+            nc.gpsimd.dma_start(out=o1_v[:, ts, :], in_=kv_sb[:, ts, 0:256])
+
+        def qb_store(half):
+            ts = slice(4 * half, 4 * half + 4)
+            nc.gpsimd.dma_start(out=o0_v[:, ts, 0:256], in_=qb_sb[:, ts, :])
+
+        rounds = [((2, 0), (3, 0), (2, 1), (3, 1))]
+        for j in (2, 3):
+            for half in range(2):
+                rounds.append(tuple((4 * (j - 1) + hh, half) for hh in range(4)))
+
+        def project(r):
+            for i, (head, half) in enumerate(rounds[r]):
+                j = 1 + head // 4
+                cols = slice(P * (head % 4), P * (head % 4) + P)
+                accs[(r, i)] = bank(i, [P, HALF], F32)
+                for g in range(PASSES):
+                    nc.tensor.matmul_mx(
+                        out=accs[(r, i)][:],
+                        lhsT=wq[j][:, g, cols].bitcast(FP8X4),
+                        lhsT_scale=ws[j][:, g, cols],
+                        rhs=xq[:, half, g, :].bitcast(FP8X4),
+                        rhs_scale=xs[:, half, g, :],
+                        start=(g == 0),
+                        stop=(g == PASSES - 1),
+                    )
+
+        def bias_rows(b):
+            for c0, c1, i in ((0, 512, b), (512, 768, b + 1)):
+                bb = bank(i, [P, c1 - c0], F32)
+                nc.tensor.matmul(out=bb[:], lhsT=ones_b[:], rhs=row_b[:, c0:c1], start=True, stop=True)
+                nc.scalar.copy(out=free_b[:, c0:c1], in_=bb[:])
 
         def bias_transpose(b):
             bt = bank(b, [P, P], BF16)
             nc.tensor.transpose(bt[:], b_raw[:], ident_b[:])
-            nc.vector.tensor_copy(out=b_t[:], in_=bt[:, 0:16])
+            nc.scalar.copy(out=b_t[:], in_=bt[:, 0:16])
+
+        def merge_tables():
+            for comp, lo, hi, dlo in COS_PARTS:
+                nc.scalar.copy(out=c_raw[:, :, dlo : dlo + hi - lo], in_=c_all[:, comp, :, lo:hi])
+            for comp, lo, hi, dlo in SIN_PARTS:
+                nc.scalar.copy(out=s_raw[:, :, dlo : dlo + hi - lo], in_=s_all[:, comp, :, lo:hi])
 
         def table_transposes(half, b):
             tb = bank(b, [P, 2, HALF], BF16)
@@ -209,102 +293,150 @@ def tile_qwen2vlattention_pa_kernel(
             nc.scalar.copy(out=tab_t[:, half, 0, :], in_=tb[:, 0, :])
             nc.scalar.activation(out=tab_t[:, half, 1, :], in_=tb[:, 1, :], func=ACT.Copy, scale=sgn[:, 0:1])
 
-        def rope(r, extras):
-            j, half = divmod(r, 2)
-            uws[r] = []
-            for hh in range(4):
-                col = bias_column(j, hh)
-                acc = accs[r][hh]
-                uw = uwp.tile([P, 2, HALF], F32, name="uw%d" % hh, tag="uw%d" % hh)
-                uws[r].append(uw)
-                if rotated(j, hh):
-                    nc.vector.scalar_tensor_tensor(
-                        out=uw[:],
-                        in0=acc[:].unsqueeze(1).to_broadcast([P, 2, HALF]),
-                        scalar=b_t[:, col : col + 1],
-                        in1=tab_t[:, half],
-                        op0=ADD,
-                        op1=MULT,
-                    )
-                else:
-                    nc.scalar.activation(
-                        out=uw[:, 0, :], in_=acc[:], func=ACT.Identity, bias=b_t[:, col : col + 1]
-                    )
-                for extra in extras[hh]:
-                    extra()
+        def rope(r, i):
+            head, half = rounds[r][i]
+            uw = uwp.tile([P, 2, HALF], F32, name="uw%d" % i, tag="uw%d" % i)
+            uws[(r, i)] = uw
+            nc.vector.scalar_tensor_tensor(
+                out=uw[:],
+                in0=accs[(r, i)][:].unsqueeze(1).to_broadcast([P, 2, HALF]),
+                scalar=b_t[:, head : head + 1],
+                in1=tab_t[:, half],
+                op0=ADD,
+                op1=MULT,
+            )
+
+        def turn(outs, uw, ts):
+            for o, t in zip(outs, ts):
+                nc.tensor.matmul(
+                    out=o, lhsT=uw[:, 0, P * t : P * t + P], rhs=ident_f[:],
+                    is_transpose=True, start=True, stop=False,
+                )
+            for o, t in zip(outs, ts):
+                nc.tensor.matmul(
+                    out=o, lhsT=uw[:, 1, P * t : P * t + P], rhs=perm_f[:],
+                    is_transpose=True, start=False, stop=True,
+                )
 
         def back(r):
-            j, half = divmod(r, 2)
+            if r == 0:
+                for half in range(2):
+                    o_ps = [bank(4 + 2 * half + tp, [P, 2, 256], F32) for tp in range(2)]
+                    for hh in range(2):
+                        cols = slice(P * hh, P * hh + P)
+                        for tt in range(2):
+                            turn([o[:, tt, cols] for o in o_ps], uws[(0, 2 * half + hh)], (tt, 2 + tt))
+                    for tp in range(2):
+                        o_sb = outp.tile([P, 2, 256], F32, name="o_sb", tag="o_sb")
+                        nc.scalar.copy(out=o_sb[:], in_=o_ps[tp][:])
+                        t8 = 4 * half + 2 * tp
+                        nc.sync.dma_start(out=o0_v[:, t8 : t8 + 2, 256:512], in_=o_sb[:])
+                return
+            half = rounds[r][0][1]
+            col = P * rounds[r][0][0]
             for tp in range(2):
                 pair = (2 * tp, 2 * tp + 1)
-                o_ps = [bank(t, [P, 512], F32) for t in pair]
+                o_ps = [bank(4 + t, [P, 512], F32) for t in pair]
                 for hh in range(4):
-                    uw = uws[r][hh]
-                    cols = slice(P * hh, P * hh + P)
-                    if rotated(j, hh):
-                        for o_t, t in zip(o_ps, pair):
-                            nc.tensor.matmul(
-                                out=o_t[:, cols], lhsT=uw[:, 0, P * t : P * t + P], rhs=ident_f[:],
-                                is_transpose=True, start=True, stop=False,
-                            )
-                        for o_t, t in zip(o_ps, pair):
-                            nc.tensor.matmul(
-                                out=o_t[:, cols], lhsT=uw[:, 1, P * t : P * t + P], rhs=perm_f[:],
-                                is_transpose=True, start=False, stop=True,
-                            )
-                    else:
-                        for o_t, t in zip(o_ps, pair):
-                            nc.tensor.transpose(o_t[:, cols], uw[:, 0, P * t : P * t + P], ident_f[:])
+                    turn([o[:, P * hh : P * hh + P] for o in o_ps], uws[(r, hh)], pair)
                 for o_t, t in zip(o_ps, pair):
-                    o_sb = outp.tile([P, 512], F32, name="o_sb", tag="o_sb")
-                    nc.scalar.copy(out=o_sb[:], in_=o_t[:])
-                    t8 = 4 * half + t
-                    if j == 0:
-                        nc.sync.dma_start(out=o1_v[:, t8, :], in_=o_sb[:, 0:256])
-                        nc.sync.dma_start(out=o2_v[:, t8, :], in_=o_sb[:, 256:512])
-                    else:
-                        nc.sync.dma_start(out=o0_v[:, t8, 512 * (j - 1) : 512 * j], in_=o_sb[:])
+                    o_sb = outp.tile([P, 2, 256], F32, name="o_sb", tag="o_sb")
+                    o_flat = o_sb[:].rearrange("p a b -> p (a b)")
+                    nc.scalar.copy(out=o_flat, in_=o_t[:])
+                    nc.sync.dma_start(out=o0_v[:, 4 * half + t, col : col + 512], in_=o_flat)
 
-        x_transposes(0, (0, 1, 2, 3, 4, 5))
-        regroup(True, 0, 0)
+        x_transposes(0, 0, (0, 1, 2), "svs")
+        regroup("v", 0, 0, 0)
+        x_transposes(0, 1, (3, 4, 5), "vsv")
+        regroup("s", 0, 0, 1)
         quant_x(0, 0)
-        regroup(True, 0, 1)
-        quant_x(0, 1)
         quant_w(0, 0)
-        regroup(True, 0, 2)
-        quant_x(0, 2)
+        for t in range(4):
+            kv_pass(0, 0, t)
+        regroup("v", 0, 1, 0)
+        regroup("s", 0, 1, 1)
+        quant_x(0, 1)
         quant_w(0, 1)
+        regroup("v", 0, 2, 0)
+        regroup("s", 0, 2, 1)
+        quant_x(0, 2)
         quant_w(0, 2)
-        project(0, (0, 1, 2, 3), True)
+        x_transposes(1, 0, (6, 7, 4), "ssv")
+        for t in range(4):
+            kv_pass(0, 1, t)
+        regroup("v", 1, 0, 0)
+        x_transposes(1, 1, (5, 6, 7), "ssv")
+        for t in range(4):
+            kv_pass(0, 2, t)
+        bias_rows(4)
         bias_transpose(6)
-        table_transposes(0, 7)
-        table_transposes(1, 6)
-        x_transposes(1, (4, 5, 7, 6, 4, 5))
-        rope(0, [[], [lambda: quant_x(1, 0)], [lambda: quant_x(1, 1)], [lambda: quant_x(1, 2)]])
-        project(1, (4, 5, 6, 7), False)
-
-        def passes_due(r):
-            if r == 0:
-                return [(1, 0), (1, 1), (1, 2)]
-            if r % 2 == 1 and (r + 3) // 2 < 4:
-                return [((r + 3) // 2, 0), ((r + 3) // 2, 1)]
-            if r % 2 == 0 and (r + 2) // 2 < 4:
-                return [((r + 2) // 2, 2)]
-            return []
-
-        def later(fn, j, g):
-            return lambda: fn(j, g)
-
-        for r in range(8):
-            extras = [[], [], [], []]
-            for k, (j, g) in enumerate(passes_due(r)):
-                if r == 0 and g == 1:
-                    extras[0].append(lambda: regroup(True, 1, 1))
-                else:
-                    regroup(False, j, g)
-                extras[k + 1].append(later(quant_w, j, g))
-            back(r)
-            if r + 1 < 8:
-                rope(r + 1, extras)
-            if r + 2 < 8:
-                project(r + 2, (4, 5, 6, 7), False)
+        for g in range(PASSES):
+            quant_x(1, g)
+        regroup("v", 1, 0, 1)
+        for g in range(1, PASSES):
+            regroup("v", 1, g, 0)
+            regroup("s", 1, g, 1)
+        for t in range(4):
+            for g in range(PASSES):
+                kv_pass(1, g, t)
+        for t in range(4):
+            kv_add(0, t)
+        merge_tables()
+        for g in range(PASSES):
+            quant_w(1, g)
+        for t in range(2):
+            kv_add(1, t)
+        table_transposes(0, 4)
+        table_transposes(1, 5)
+        project(0)
+        for g in range(2):
+            for part in range(2):
+                regroup("s", 2, g, part)
+        for part in range(2):
+            regroup("g", 2, 2, part)
+        for tp in range(2):
+            free_rope(kv_sb, tp)
+        for t in range(2, 4):
+            kv_add(1, t)
+        v_store(0)
+        v_store(1)
+        for i in range(4):
+            rope(0, i)
+        for tp in range(4):
+            qb_project(tp)
+        for g in range(PASSES):
+            quant_w(2, g)
+        for tp in range(2, 4):
+            free_rope(kv_sb, tp)
+        for tp in range(4):
+            qb_add(tp)
+        for tp in range(4):
+            free_rope(qb_sb, tp)
+        project(1)
+        for g in range(2):
+            for part in range(2):
+                regroup("s", 3, g, part)
+        back(0)
+        for part in range(2):
+            regroup("s", 3, 2, part)
+        for i in range(4):
+            rope(1, i)
+        for g in range(PASSES):
+            quant_w(3, g)
+        project(2)
+        back(1)
+        k_store(0)
+        for i in range(4):
+            rope(2, i)
+        project(3)
+        back(2)
+        k_store(1)
+        for i in range(4):
+            rope(3, i)
+        project(4)
+        back(3)
+        qb_store(0)
+        qb_store(1)
+        for i in range(4):
+            rope(4, i)
+        back(4)

@@ -48,7 +48,7 @@ def tile_qwen2vlattention_pa_kernel(
         wgp = ctx.enter_context(tc.tile_pool(name="wgp", bufs=4))
         uwp = ctx.enter_context(tc.tile_pool(name="uwp", bufs=2))
         krp = ctx.enter_context(tc.tile_pool(name="krp", bufs=2))
-        outp = ctx.enter_context(tc.tile_pool(name="outp", bufs=6))
+        outp = ctx.enter_context(tc.tile_pool(name="outp", bufs=8))
         psum = ctx.enter_context(tc.psum_pool(name="psum", bufs=1))
         ctx.enter_context(tc.manual_schedule())
 
@@ -63,9 +63,8 @@ def tile_qwen2vlattention_pa_kernel(
         warm = keep.tile([P, 1], F32, name="warm")
         b_raw = keep.tile([P, P], BF16, name="b_raw")
         b_t = keep.tile([P, 16], F32, name="b_t")
-        row_b = keep.tile([P, 768], BF16, name="row_b")
-        free_b = keep.tile([P, 768], F32, name="free_b")
-        qb_sb = keep.tile([P, T8, 256], F32, name="qb_sb")
+        row_b = keep.tile([P, 512], BF16, name="row_b")
+        free_b = keep.tile([P, 512], F32, name="free_b")
         kv_sb = keep.tile([P, T8, 512], F32, name="kv_sb")
         c_all = keep.tile([P, 3, T8, P], BF16, name="c_all")
         s_all = keep.tile([P, 3, T8, P], BF16, name="s_all")
@@ -122,7 +121,6 @@ def tile_qwen2vlattention_pa_kernel(
         load_x(0)
         nc.gpsimd.dma_start(out=row_b[0:1, 0:256], in_=bk.rearrange("(o h) d -> o (h d)", o=1))
         nc.gpsimd.dma_start(out=row_b[0:1, 256:512], in_=bv.rearrange("(o h) d -> o (h d)", o=1))
-        nc.gpsimd.dma_start(out=row_b[0:1, 512:768], in_=bq[0:2, :].rearrange("(o h) d -> o (h d)", o=1))
         nc.gpsimd.dma_start(out=b_raw[0:12, :], in_=bq)
         load_w(0)
         load_x(1)
@@ -177,7 +175,6 @@ def tile_qwen2vlattention_pa_kernel(
             )
 
         kv_acc = {}
-        qb_acc = {}
 
         def kv_pass(half, g, t):
             if g == 0:
@@ -198,30 +195,6 @@ def tile_qwen2vlattention_pa_kernel(
                 out=kv_sb[:, 4 * half + t, :], in0=kv_acc[(half, t)][:], in1=free_b[:, 0:512], op=ADD
             )
 
-        def qb_project(tp):
-            qb_acc[tp] = bank(4 + tp, [P, 2, 256], F32)
-            for tt in range(2):
-                half, t = divmod(2 * tp + tt, 4)
-                tok = slice(P * t, P * t + P)
-                for g in range(PASSES):
-                    nc.tensor.matmul_mx(
-                        out=qb_acc[tp][:, tt, :],
-                        lhsT=xq[:, half, g, tok].bitcast(FP8X4),
-                        lhsT_scale=xs[:, half, g, tok],
-                        rhs=wq[1][:, g, 0:256].bitcast(FP8X4),
-                        rhs_scale=ws[1][:, g, 0:256],
-                        start=(g == 0),
-                        stop=(g == PASSES - 1),
-                    )
-
-        def qb_add(tp):
-            nc.vector.tensor_tensor(
-                out=qb_sb[:, 2 * tp : 2 * tp + 2, :],
-                in0=qb_acc[tp][:],
-                in1=free_b[:, 512:768].unsqueeze(1).to_broadcast([P, 2, 256]),
-                op=ADD,
-            )
-
         def v_store(half):
             ts = slice(4 * half, 4 * half + 4)
             nc.sync.dma_start(out=o2_v[:, ts, :], in_=kv_sb[:, ts, 256:512])
@@ -240,14 +213,10 @@ def tile_qwen2vlattention_pa_kernel(
 
         def k_store(half):
             ts = slice(4 * half, 4 * half + 4)
-            nc.gpsimd.dma_start(out=o1_v[:, ts, :], in_=kv_sb[:, ts, 0:256])
+            nc.sync.dma_start(out=o1_v[:, ts, :], in_=kv_sb[:, ts, 0:256])
 
-        def qb_store(half):
-            ts = slice(4 * half, 4 * half + 4)
-            nc.gpsimd.dma_start(out=o0_v[:, ts, 0:256], in_=qb_sb[:, ts, :])
-
-        rounds = [((2, 0), (3, 0), (2, 1), (3, 1))]
-        for j in (2, 3):
+        rounds = []
+        for j in (1, 2, 3):
             for half in range(2):
                 rounds.append(tuple((4 * (j - 1) + hh, half) for hh in range(4)))
 
@@ -255,7 +224,7 @@ def tile_qwen2vlattention_pa_kernel(
             for i, (head, half) in enumerate(rounds[r]):
                 j = 1 + head // 4
                 cols = slice(P * (head % 4), P * (head % 4) + P)
-                accs[(r, i)] = bank(i, [P, HALF], F32)
+                accs[(r, i)] = bank((2, 3, 0, 1)[i] if r == 0 else 4 + i, [P, HALF], F32)
                 for g in range(PASSES):
                     nc.tensor.matmul_mx(
                         out=accs[(r, i)][:],
@@ -268,10 +237,9 @@ def tile_qwen2vlattention_pa_kernel(
                     )
 
         def bias_rows(b):
-            for c0, c1, i in ((0, 512, b), (512, 768, b + 1)):
-                bb = bank(i, [P, c1 - c0], F32)
-                nc.tensor.matmul(out=bb[:], lhsT=ones_b[:], rhs=row_b[:, c0:c1], start=True, stop=True)
-                nc.scalar.copy(out=free_b[:, c0:c1], in_=bb[:])
+            bb = bank(b, [P, 512], F32)
+            nc.tensor.matmul(out=bb[:], lhsT=ones_b[:], rhs=row_b[:], start=True, stop=True)
+            nc.scalar.copy(out=free_b[:], in_=bb[:])
 
         def bias_transpose(b):
             bt = bank(b, [P, P], BF16)
@@ -318,32 +286,18 @@ def tile_qwen2vlattention_pa_kernel(
                     is_transpose=True, start=False, stop=True,
                 )
 
-        def back(r):
-            if r == 0:
-                for half in range(2):
-                    o_ps = [bank(4 + 2 * half + tp, [P, 2, 256], F32) for tp in range(2)]
-                    for hh in range(2):
-                        cols = slice(P * hh, P * hh + P)
-                        for tt in range(2):
-                            turn([o[:, tt, cols] for o in o_ps], uws[(0, 2 * half + hh)], (tt, 2 + tt))
-                    for tp in range(2):
-                        o_sb = outp.tile([P, 2, 256], F32, name="o_sb", tag="o_sb")
-                        nc.scalar.copy(out=o_sb[:], in_=o_ps[tp][:])
-                        t8 = 4 * half + 2 * tp
-                        nc.sync.dma_start(out=o0_v[:, t8 : t8 + 2, 256:512], in_=o_sb[:])
-                return
+        def back(r, engines="ssss"):
             half = rounds[r][0][1]
             col = P * rounds[r][0][0]
             for tp in range(2):
                 pair = (2 * tp, 2 * tp + 1)
-                o_ps = [bank(4 + t, [P, 512], F32) for t in pair]
+                o_ps = [bank(t, [P, 512], F32) for t in pair]
                 for hh in range(4):
                     turn([o[:, P * hh : P * hh + P] for o in o_ps], uws[(r, hh)], pair)
                 for o_t, t in zip(o_ps, pair):
-                    o_sb = outp.tile([P, 2, 256], F32, name="o_sb", tag="o_sb")
-                    o_flat = o_sb[:].rearrange("p a b -> p (a b)")
-                    nc.scalar.copy(out=o_flat, in_=o_t[:])
-                    nc.sync.dma_start(out=o0_v[:, 4 * half + t, col : col + 512], in_=o_flat)
+                    o_sb = outp.tile([P, 512], F32, name="o_sb", tag="o_sb")
+                    copy_on(engines[t], o_sb[:], o_t[:])
+                    nc.sync.dma_start(out=o0_v[:, 4 * half + t, col : col + 512], in_=o_sb[:])
 
         x_transposes(0, 0, (0, 1, 2), "svs")
         regroup("v", 0, 0, 0)
@@ -361,18 +315,18 @@ def tile_qwen2vlattention_pa_kernel(
         regroup("s", 0, 2, 1)
         quant_x(0, 2)
         quant_w(0, 2)
-        x_transposes(1, 0, (6, 7, 4), "ssv")
+        x_transposes(1, 0, (6, 7, 4), "sss")
         for t in range(4):
             kv_pass(0, 1, t)
         regroup("v", 1, 0, 0)
-        x_transposes(1, 1, (5, 6, 7), "ssv")
+        x_transposes(1, 1, (5, 6, 7), "sss")
         for t in range(4):
             kv_pass(0, 2, t)
         bias_rows(4)
         bias_transpose(6)
+        regroup("v", 1, 0, 1)
         for g in range(PASSES):
             quant_x(1, g)
-        regroup("v", 1, 0, 1)
         for g in range(1, PASSES):
             regroup("v", 1, g, 0)
             regroup("s", 1, g, 1)
@@ -384,59 +338,53 @@ def tile_qwen2vlattention_pa_kernel(
         merge_tables()
         for g in range(PASSES):
             quant_w(1, g)
-        for t in range(2):
-            kv_add(1, t)
-        table_transposes(0, 4)
-        table_transposes(1, 5)
+        table_transposes(0, 0)
+        table_transposes(1, 1)
         project(0)
-        for g in range(2):
+        for t in range(4):
+            kv_add(1, t)
+        for g in range(PASSES):
             for part in range(2):
                 regroup("s", 2, g, part)
-        for part in range(2):
-            regroup("g", 2, 2, part)
-        for tp in range(2):
-            free_rope(kv_sb, tp)
-        for t in range(2, 4):
-            kv_add(1, t)
         v_store(0)
         v_store(1)
         for i in range(4):
             rope(0, i)
         for tp in range(4):
-            qb_project(tp)
-        for g in range(PASSES):
-            quant_w(2, g)
-        for tp in range(2, 4):
             free_rope(kv_sb, tp)
-        for tp in range(4):
-            qb_add(tp)
-        for tp in range(4):
-            free_rope(qb_sb, tp)
         project(1)
+        back(0)
+        for g in range(2):
+            quant_w(2, g)
+        rope(1, 0)
+        quant_w(2, 2)
+        for i in range(1, 4):
+            rope(1, i)
         for g in range(2):
             for part in range(2):
                 regroup("s", 3, g, part)
-        back(0)
+        project(2)
+        back(1)
         for part in range(2):
             regroup("s", 3, 2, part)
         for i in range(4):
-            rope(1, i)
-        for g in range(PASSES):
-            quant_w(3, g)
-        project(2)
-        back(1)
-        k_store(0)
-        for i in range(4):
             rope(2, i)
+        for g in range(2):
+            quant_w(3, g)
         project(3)
         back(2)
-        k_store(1)
         for i in range(4):
             rope(3, i)
+            if i == 1:
+                quant_w(3, 2)
         project(4)
         back(3)
-        qb_store(0)
-        qb_store(1)
+        k_store(0)
+        k_store(1)
         for i in range(4):
             rope(4, i)
+        project(5)
         back(4)
+        for i in range(4):
+            rope(5, i)
+        back(5, "svsv")

@@ -199,17 +199,16 @@ def tile_qwen2vlattention_pa_kernel(
             ts = slice(4 * half, 4 * half + 4)
             nc.sync.dma_start(out=o2_v[:, ts, :], in_=kv_sb[:, ts, 256:512])
 
-        def free_rope(tile, tp):
-            ts = slice(2 * tp, 2 * tp + 2)
-            y = tile[:, ts, 0:256].rearrange("p t (h d) -> p t h d", h=2)
-            c_b = c_raw[:, ts, :].unsqueeze(2).to_broadcast([P, 2, 2, P])
-            s_b = s_raw[:, ts, :].unsqueeze(2).to_broadcast([P, 2, 2, P])
-            a = krp.tile([P, 2, 2, P], F32, name="ka", tag="ka")
-            w = krp.tile([P, 2, 2, P], F32, name="kw", tag="kw")
+        def k_rope(t8):
+            y = kv_sb[:, t8, 0:256].rearrange("p (h d) -> p h d", h=2)
+            c_b = c_raw[:, t8, :].unsqueeze(1).to_broadcast([P, 2, P])
+            s_b = s_raw[:, t8, :].unsqueeze(1).to_broadcast([P, 2, P])
+            a = krp.tile([P, 2, P], F32, name="ka", tag="ka")
+            w = krp.tile([P, 2, P], F32, name="kw", tag="kw")
             nc.gpsimd.tensor_tensor(out=a[:], in0=y, in1=c_b, op=MULT)
             nc.gpsimd.tensor_tensor(out=w[:], in0=y, in1=s_b, op=MULT)
-            nc.gpsimd.tensor_tensor(out=y[:, :, :, 0:64], in0=a[:, :, :, 0:64], in1=w[:, :, :, 64:128], op=SUB)
-            nc.gpsimd.tensor_tensor(out=y[:, :, :, 64:128], in0=a[:, :, :, 64:128], in1=w[:, :, :, 0:64], op=ADD)
+            nc.gpsimd.tensor_tensor(out=y[:, :, 0:64], in0=a[:, :, 0:64], in1=w[:, :, 64:128], op=SUB)
+            nc.gpsimd.tensor_tensor(out=y[:, :, 64:128], in0=a[:, :, 64:128], in1=w[:, :, 0:64], op=ADD)
 
         def k_store(half):
             ts = slice(4 * half, 4 * half + 4)
@@ -350,8 +349,8 @@ def tile_qwen2vlattention_pa_kernel(
         v_store(1)
         for i in range(4):
             rope(0, i)
-        for tp in range(4):
-            free_rope(kv_sb, tp)
+        for t8 in (4, 5, 6, 7, 0, 1, 2, 3):
+            k_rope(t8)
         project(1)
         back(0)
         for g in range(2):

@@ -48,7 +48,7 @@ def tile_qwen2vlattention_pa_kernel(
         wgp = ctx.enter_context(tc.tile_pool(name="wgp", bufs=4))
         uwp = ctx.enter_context(tc.tile_pool(name="uwp", bufs=2))
         krp = ctx.enter_context(tc.tile_pool(name="krp", bufs=2))
-        outp = ctx.enter_context(tc.tile_pool(name="outp", bufs=8))
+        outp = ctx.enter_context(tc.tile_pool(name="outp", bufs=7))
         psum = ctx.enter_context(tc.psum_pool(name="psum", bufs=1))
         ctx.enter_context(tc.manual_schedule())
 
@@ -60,11 +60,13 @@ def tile_qwen2vlattention_pa_kernel(
         perm_f = keep.tile([P, P], F32, name="perm_f")
         ones_b = keep.tile([P, P], BF16, name="ones_b")
         sgn = keep.tile([P, 1], F32, name="sgn")
+        busy = keep.tile([P, 512], BF16, name="busy")
         warm = keep.tile([P, 1], F32, name="warm")
         b_raw = keep.tile([P, P], BF16, name="b_raw")
         b_t = keep.tile([P, 16], F32, name="b_t")
-        row_b = keep.tile([P, 512], BF16, name="row_b")
-        free_b = keep.tile([P, 512], F32, name="free_b")
+        row_b = keep.tile([P, 768], BF16, name="row_b")
+        free_b = keep.tile([P, 768], F32, name="free_b")
+        qb_sb = keep.tile([P, T8, 256], F32, name="qb_sb")
         kv_sb = keep.tile([P, T8, 512], F32, name="kv_sb")
         c_all = keep.tile([P, 3, T8, P], BF16, name="c_all")
         s_all = keep.tile([P, 3, T8, P], BF16, name="s_all")
@@ -82,6 +84,7 @@ def tile_qwen2vlattention_pa_kernel(
         ]
         x_w = x_raw[:].bitcast(F32)
 
+        nc.vector.memset(busy[:], 0.0)
         nc.vector.memset(sgn[0:64, :], 1.0)
         nc.vector.memset(sgn[64:128, :], -1.0)
         nc.scalar.copy(out=warm[:], in_=sgn[:])
@@ -121,6 +124,7 @@ def tile_qwen2vlattention_pa_kernel(
         load_x(0)
         nc.gpsimd.dma_start(out=row_b[0:1, 0:256], in_=bk.rearrange("(o h) d -> o (h d)", o=1))
         nc.gpsimd.dma_start(out=row_b[0:1, 256:512], in_=bv.rearrange("(o h) d -> o (h d)", o=1))
+        nc.gpsimd.dma_start(out=row_b[0:1, 512:768], in_=bq[0:2, :].rearrange("(o h) d -> o (h d)", o=1))
         nc.gpsimd.dma_start(out=b_raw[0:12, :], in_=bq)
         load_w(0)
         load_x(1)
@@ -175,6 +179,7 @@ def tile_qwen2vlattention_pa_kernel(
             )
 
         kv_acc = {}
+        qb_acc = {}
 
         def kv_pass(half, g, t):
             if g == 0:
@@ -195,27 +200,56 @@ def tile_qwen2vlattention_pa_kernel(
                 out=kv_sb[:, 4 * half + t, :], in0=kv_acc[(half, t)][:], in1=free_b[:, 0:512], op=ADD
             )
 
+        def qb_project(tp):
+            qb_acc[tp] = bank(4 + tp, [P, 2, 256], F32)
+            for tt in range(2):
+                half, t = divmod(2 * tp + tt, 4)
+                tok = slice(P * t, P * t + P)
+                for g in range(PASSES):
+                    nc.tensor.matmul_mx(
+                        out=qb_acc[tp][:, tt, :],
+                        lhsT=xq[:, half, g, tok].bitcast(FP8X4),
+                        lhsT_scale=xs[:, half, g, tok],
+                        rhs=wq[1][:, g, 0:256].bitcast(FP8X4),
+                        rhs_scale=ws[1][:, g, 0:256],
+                        start=(g == 0),
+                        stop=(g == PASSES - 1),
+                    )
+
+        def qb_add(tp):
+            nc.vector.tensor_tensor(
+                out=qb_sb[:, 2 * tp : 2 * tp + 2, :],
+                in0=qb_acc[tp][:],
+                in1=free_b[:, 512:768].unsqueeze(1).to_broadcast([P, 2, 256]),
+                op=ADD,
+            )
+
         def v_store(half):
             ts = slice(4 * half, 4 * half + 4)
             nc.sync.dma_start(out=o2_v[:, ts, :], in_=kv_sb[:, ts, 256:512])
 
-        def k_rope(t8):
-            y = kv_sb[:, t8, 0:256].rearrange("p (h d) -> p h d", h=2)
-            c_b = c_raw[:, t8, :].unsqueeze(1).to_broadcast([P, 2, P])
-            s_b = s_raw[:, t8, :].unsqueeze(1).to_broadcast([P, 2, P])
-            a = krp.tile([P, 2, P], F32, name="ka", tag="ka")
-            w = krp.tile([P, 2, P], F32, name="kw", tag="kw")
+        def free_rope(tile, tp):
+            ts = slice(2 * tp, 2 * tp + 2)
+            y = tile[:, ts, 0:256].rearrange("p t (h d) -> p t h d", h=2)
+            c_b = c_raw[:, ts, :].unsqueeze(2).to_broadcast([P, 2, 2, P])
+            s_b = s_raw[:, ts, :].unsqueeze(2).to_broadcast([P, 2, 2, P])
+            a = krp.tile([P, 2, 2, P], F32, name="ka", tag="ka")
+            w = krp.tile([P, 2, 2, P], F32, name="kw", tag="kw")
             nc.gpsimd.tensor_tensor(out=a[:], in0=y, in1=c_b, op=MULT)
             nc.gpsimd.tensor_tensor(out=w[:], in0=y, in1=s_b, op=MULT)
-            nc.gpsimd.tensor_tensor(out=y[:, :, 0:64], in0=a[:, :, 0:64], in1=w[:, :, 64:128], op=SUB)
-            nc.gpsimd.tensor_tensor(out=y[:, :, 64:128], in0=a[:, :, 64:128], in1=w[:, :, 0:64], op=ADD)
+            nc.gpsimd.tensor_tensor(out=y[:, :, :, 0:64], in0=a[:, :, :, 0:64], in1=w[:, :, :, 64:128], op=SUB)
+            nc.gpsimd.tensor_tensor(out=y[:, :, :, 64:128], in0=a[:, :, :, 64:128], in1=w[:, :, :, 0:64], op=ADD)
+
+        def qb_store(half):
+            ts = slice(4 * half, 4 * half + 4)
+            nc.sync.dma_start(out=o0_v[:, ts, 0:256], in_=qb_sb[:, ts, :])
 
         def k_store(half):
             ts = slice(4 * half, 4 * half + 4)
             nc.sync.dma_start(out=o1_v[:, ts, :], in_=kv_sb[:, ts, 0:256])
 
-        rounds = []
-        for j in (1, 2, 3):
+        rounds = [((2, 0), (3, 0), (2, 1), (3, 1))]
+        for j in (2, 3):
             for half in range(2):
                 rounds.append(tuple((4 * (j - 1) + hh, half) for hh in range(4)))
 
@@ -235,10 +269,16 @@ def tile_qwen2vlattention_pa_kernel(
                         stop=(g == PASSES - 1),
                     )
 
+        def keep_clock(n, b):
+            for i in range(n):
+                spare = bank(b, [P, 512], F32)
+                nc.tensor.matmul(out=spare[:], lhsT=busy[:, 0:P], rhs=busy[:], start=True, stop=True)
+
         def bias_rows(b):
-            bb = bank(b, [P, 512], F32)
-            nc.tensor.matmul(out=bb[:], lhsT=ones_b[:], rhs=row_b[:], start=True, stop=True)
-            nc.scalar.copy(out=free_b[:], in_=bb[:])
+            for c0, c1, i in ((0, 512, b), (512, 768, b + 1)):
+                bb = bank(i, [P, c1 - c0], F32)
+                nc.tensor.matmul(out=bb[:], lhsT=ones_b[:], rhs=row_b[:, c0:c1], start=True, stop=True)
+                nc.scalar.copy(out=free_b[:, c0:c1], in_=bb[:])
 
         def bias_transpose(b):
             bt = bank(b, [P, P], BF16)
@@ -286,6 +326,20 @@ def tile_qwen2vlattention_pa_kernel(
                 )
 
         def back(r, engines="ssss"):
+            if r == 0:
+                for half in range(2):
+                    o_ps = [bank(2 * half + tp, [P, 2, 256], F32) for tp in range(2)]
+                    for hh in range(2):
+                        cols = slice(P * hh, P * hh + P)
+                        for tt in range(2):
+                            turn([o[:, tt, cols] for o in o_ps], uws[(0, 2 * half + hh)], (tt, 2 + tt))
+                    for tp in range(2):
+                        o_sb = outp.tile([P, 512], F32, name="o_sb", tag="o_sb")
+                        o_v = o_sb[:].rearrange("p (a b) -> p a b", a=2)
+                        copy_on("s", o_v, o_ps[tp][:])
+                        t8 = 4 * half + 2 * tp
+                        nc.sync.dma_start(out=o0_v[:, t8 : t8 + 2, 256:512], in_=o_v)
+                return
             half = rounds[r][0][1]
             col = P * rounds[r][0][0]
             for tp in range(2):
@@ -298,9 +352,11 @@ def tile_qwen2vlattention_pa_kernel(
                     copy_on(engines[t], o_sb[:], o_t[:])
                     nc.sync.dma_start(out=o0_v[:, 4 * half + t, col : col + 512], in_=o_sb[:])
 
+        keep_clock(4, 7)
         x_transposes(0, 0, (0, 1, 2), "svs")
         regroup("v", 0, 0, 0)
         x_transposes(0, 1, (3, 4, 5), "vsv")
+        keep_clock(3, 7)
         regroup("s", 0, 0, 1)
         quant_x(0, 0)
         quant_w(0, 0)
@@ -349,41 +405,42 @@ def tile_qwen2vlattention_pa_kernel(
         v_store(1)
         for i in range(4):
             rope(0, i)
-        for t8 in (4, 5, 6, 7, 0, 1, 2, 3):
-            k_rope(t8)
-        project(1)
+        for tp in (2, 3, 0, 1):
+            free_rope(kv_sb, tp)
+        for tp in range(4):
+            qb_project(tp)
         back(0)
         for g in range(2):
             quant_w(2, g)
-        rope(1, 0)
+        for tp in range(4):
+            qb_add(tp)
+        for tp in range(4):
+            free_rope(qb_sb, tp)
         quant_w(2, 2)
-        for i in range(1, 4):
+        project(1)
+        for i in range(4):
             rope(1, i)
-        for g in range(2):
+        for g in range(PASSES):
             for part in range(2):
                 regroup("s", 3, g, part)
         project(2)
         back(1)
-        for part in range(2):
-            regroup("s", 3, 2, part)
-        for i in range(4):
-            rope(2, i)
         for g in range(2):
             quant_w(3, g)
-        project(3)
-        back(2)
         for i in range(4):
-            rope(3, i)
+            rope(2, i)
             if i == 1:
                 quant_w(3, 2)
-        project(4)
-        back(3)
+        project(3)
+        back(2)
         k_store(0)
         k_store(1)
         for i in range(4):
-            rope(4, i)
-        project(5)
-        back(4)
+            rope(3, i)
+        project(4)
+        back(3)
+        qb_store(0)
         for i in range(4):
-            rope(5, i)
-        back(5, "svsv")
+            rope(4, i)
+        back(4, "svsv")
+        qb_store(1)

@@ -63,9 +63,8 @@ def tile_qwen2vlattention_pa_kernel(
         busy = keep.tile([P, 512], BF16, name="busy")
         warm = keep.tile([P, 1], F32, name="warm")
         b_raw = keep.tile([P, P], BF16, name="b_raw")
-        b_t = keep.tile([P, 16], F32, name="b_t")
         row_b = keep.tile([P, 768], BF16, name="row_b")
-        free_b = keep.tile([P, 768], F32, name="free_b")
+        free_b = keep.tile([P, 784], F32, name="free_b")
         qb_sb = keep.tile([P, T8, 256], F32, name="qb_sb")
         kv_sb = keep.tile([P, T8, 512], F32, name="kv_sb")
         c_all = keep.tile([P, 3, T8, P], BF16, name="c_all")
@@ -104,8 +103,8 @@ def tile_qwen2vlattention_pa_kernel(
                     in_=x_v[:, t8 : t8 + 2, :].rearrange("p t m -> p (t m)"),
                 )
 
-        def load_w(j):
-            for g in range(PASSES):
+        def load_w(j, passes=range(PASSES)):
+            for g in passes:
                 rows = slice(512 * g, 512 * g + 512)
                 if j == 0:
                     sources = (wk_v[rows, :], wv_v[rows, :])
@@ -121,13 +120,14 @@ def tile_qwen2vlattention_pa_kernel(
             for table, view in ((c_all, cos_v), (s_all, sin_v)):
                 nc.sync.dma_start(out=table[:], in_=view.rearrange("c (p t) d -> p c t d", t=T8))
 
+        nc.scalar.dma_start(out=row_b[0:1, 0:256], in_=bk.rearrange("(o h) d -> o (h d)", o=1))
+        nc.scalar.dma_start(out=row_b[0:1, 256:512], in_=bv.rearrange("(o h) d -> o (h d)", o=1))
+        nc.scalar.dma_start(out=row_b[0:1, 512:768], in_=bq[4:6, :].rearrange("(o h) d -> o (h d)", o=1))
+        nc.scalar.dma_start(out=b_raw[0:12, :], in_=bq)
+        load_w(0, (0,))
         load_x(0)
-        nc.gpsimd.dma_start(out=row_b[0:1, 0:256], in_=bk.rearrange("(o h) d -> o (h d)", o=1))
-        nc.gpsimd.dma_start(out=row_b[0:1, 256:512], in_=bv.rearrange("(o h) d -> o (h d)", o=1))
-        nc.gpsimd.dma_start(out=row_b[0:1, 512:768], in_=bq[0:2, :].rearrange("(o h) d -> o (h d)", o=1))
-        nc.gpsimd.dma_start(out=b_raw[0:12, :], in_=bq)
-        load_w(0)
         load_x(1)
+        load_w(0, (1, 2))
         load_w(1)
         load_tables()
         load_w(2)
@@ -146,17 +146,22 @@ def tile_qwen2vlattention_pa_kernel(
             else:
                 nc.gpsimd.tensor_scalar(out=out, in0=in_, scalar1=1.0, scalar2=0.0, op0=MULT, op1=ADD)
 
-        def x_transposes(half, tp, banks, engines):
+        x_ps = {}
+
+        def x_turn(half, tp, banks):
             for g in range(PASSES):
-                if tp == 0:
-                    xg[(half, g)] = xgp.tile([P, 2048], BF16, name="xg", tag="xg", align_bytes=64)
-                words = xg[(half, g)][:].bitcast(F32).rearrange("p (tt s u) -> p tt s u", tt=4, u=2)
                 xt = bank(banks[g], [P, 2, 2, P], F32)
+                x_ps[(half, tp, g)] = xt
                 for tt in range(2):
                     for u in range(2):
                         col = (4 * half + 2 * tp + tt) * (M // 2) + 256 * g
                         nc.tensor.transpose(xt[:, tt, u, :], x_w[:, col + u : col + 256 : 2], ident_f[:])
-                copy_on(engines[g], words[:, 2 * tp : 2 * tp + 2], xt[:].rearrange("p tt u s -> p tt s u"))
+
+        def x_copy(engine, half, tp, g):
+            if (half, g) not in xg:
+                xg[(half, g)] = xgp.tile([P, 2048], BF16, name="xg", tag="xg", align_bytes=64)
+            words = xg[(half, g)][:].bitcast(F32).rearrange("p (tt s u) -> p tt s u", tt=4, u=2)
+            copy_on(engine, words[:, 2 * tp : 2 * tp + 2], x_ps[(half, tp, g)][:].rearrange("p tt u s -> p tt s u"))
 
         def quant_x(half, g):
             nc.vector.quantize_mx(
@@ -164,7 +169,7 @@ def tile_qwen2vlattention_pa_kernel(
             )
 
         def regroup(engine, j, g, part):
-            if part == 0:
+            if (j, g) not in wg:
                 wg[(j, g)] = wgp.tile([P, 2048], BF16, name="wg", tag="wg", align_bytes=64)
             dst = wg[(j, g)][:, 1024 * part : 1024 * part + 1024].rearrange("p (c i t) -> p c t i", i=4, t=4)
             if j == 0:
@@ -201,7 +206,7 @@ def tile_qwen2vlattention_pa_kernel(
             )
 
         def qb_project(tp):
-            qb_acc[tp] = bank(4 + tp, [P, 2, 256], F32)
+            qb_acc[tp] = bank((6, 7, 4, 5)[tp], [P, 2, 256], F32)
             for tt in range(2):
                 half, t = divmod(2 * tp + tt, 4)
                 tok = slice(P * t, P * t + P)
@@ -210,8 +215,8 @@ def tile_qwen2vlattention_pa_kernel(
                         out=qb_acc[tp][:, tt, :],
                         lhsT=xq[:, half, g, tok].bitcast(FP8X4),
                         lhsT_scale=xs[:, half, g, tok],
-                        rhs=wq[1][:, g, 0:256].bitcast(FP8X4),
-                        rhs_scale=ws[1][:, g, 0:256],
+                        rhs=wq[2][:, g, 0:256].bitcast(FP8X4),
+                        rhs_scale=ws[2][:, g, 0:256],
                         start=(g == 0),
                         stop=(g == PASSES - 1),
                     )
@@ -240,24 +245,23 @@ def tile_qwen2vlattention_pa_kernel(
             nc.gpsimd.tensor_tensor(out=y[:, :, :, 0:64], in0=a[:, :, :, 0:64], in1=w[:, :, :, 64:128], op=SUB)
             nc.gpsimd.tensor_tensor(out=y[:, :, :, 64:128], in0=a[:, :, :, 64:128], in1=w[:, :, :, 0:64], op=ADD)
 
-        def qb_store(half):
-            ts = slice(4 * half, 4 * half + 4)
-            nc.sync.dma_start(out=o0_v[:, ts, 0:256], in_=qb_sb[:, ts, :])
+        def qb_store(tp):
+            ts = slice(2 * tp, 2 * tp + 2)
+            nc.sync.dma_start(out=o0_v[:, ts, 512:768], in_=qb_sb[:, ts, :])
 
         def k_store(half):
             ts = slice(4 * half, 4 * half + 4)
             nc.sync.dma_start(out=o1_v[:, ts, :], in_=kv_sb[:, ts, 0:256])
 
-        rounds = [((2, 0), (3, 0), (2, 1), (3, 1))]
-        for j in (2, 3):
-            for half in range(2):
-                rounds.append(tuple((4 * (j - 1) + hh, half) for hh in range(4)))
+        rounds = [tuple((hh, half) for hh in range(4)) for half in range(2)]
+        rounds.append(((6, 0), (7, 0), (6, 1), (7, 1)))
+        rounds += [tuple((8 + hh, half) for hh in range(4)) for half in range(2)]
 
         def project(r):
             for i, (head, half) in enumerate(rounds[r]):
                 j = 1 + head // 4
                 cols = slice(P * (head % 4), P * (head % 4) + P)
-                accs[(r, i)] = bank((2, 3, 0, 1)[i] if r == 0 else 4 + i, [P, HALF], F32)
+                accs[(r, i)] = bank(i if r == 0 else (6, 7, 4, 5)[i], [P, HALF], F32)
                 for g in range(PASSES):
                     nc.tensor.matmul_mx(
                         out=accs[(r, i)][:],
@@ -274,16 +278,16 @@ def tile_qwen2vlattention_pa_kernel(
                 spare = bank(b, [P, 512], F32)
                 nc.tensor.matmul(out=spare[:], lhsT=busy[:, 0:P], rhs=busy[:], start=True, stop=True)
 
-        def bias_rows(b):
-            for c0, c1, i in ((0, 512, b), (512, 768, b + 1)):
-                bb = bank(i, [P, c1 - c0], F32)
-                nc.tensor.matmul(out=bb[:], lhsT=ones_b[:], rhs=row_b[:, c0:c1], start=True, stop=True)
-                nc.scalar.copy(out=free_b[:, c0:c1], in_=bb[:])
+        def bias_turn(b):
+            bias_ps = [bank(b, [P, 512], F32), bank(b + 1, [P, 272], F32)]
+            nc.tensor.matmul(out=bias_ps[0][:], lhsT=ones_b[:], rhs=row_b[:, 0:512], start=True, stop=True)
+            nc.tensor.matmul(out=bias_ps[1][:, 0:256], lhsT=ones_b[:], rhs=row_b[:, 512:768], start=True, stop=True)
+            nc.tensor.matmul(out=bias_ps[1][:, 256:272], lhsT=b_raw[:], rhs=ident_b[:, 0:16], start=True, stop=True)
+            return bias_ps
 
-        def bias_transpose(b):
-            bt = bank(b, [P, P], BF16)
-            nc.tensor.transpose(bt[:], b_raw[:], ident_b[:])
-            nc.scalar.copy(out=b_t[:], in_=bt[:, 0:16])
+        def bias_copy(bias_ps):
+            nc.scalar.copy(out=free_b[:, 0:512], in_=bias_ps[0][:])
+            nc.scalar.copy(out=free_b[:, 512:784], in_=bias_ps[1][:])
 
         def merge_tables():
             for comp, lo, hi, dlo in COS_PARTS:
@@ -307,7 +311,7 @@ def tile_qwen2vlattention_pa_kernel(
             nc.vector.scalar_tensor_tensor(
                 out=uw[:],
                 in0=accs[(r, i)][:].unsqueeze(1).to_broadcast([P, 2, HALF]),
-                scalar=b_t[:, head : head + 1],
+                scalar=free_b[:, 768 + head : 769 + head],
                 in1=tab_t[:, half],
                 op0=ADD,
                 op1=MULT,
@@ -326,19 +330,19 @@ def tile_qwen2vlattention_pa_kernel(
                 )
 
         def back(r, engines="ssss"):
-            if r == 0:
+            if r == 2:
                 for half in range(2):
                     o_ps = [bank(2 * half + tp, [P, 2, 256], F32) for tp in range(2)]
                     for hh in range(2):
                         cols = slice(P * hh, P * hh + P)
                         for tt in range(2):
-                            turn([o[:, tt, cols] for o in o_ps], uws[(0, 2 * half + hh)], (tt, 2 + tt))
+                            turn([o[:, tt, cols] for o in o_ps], uws[(2, 2 * half + hh)], (tt, 2 + tt))
                     for tp in range(2):
                         o_sb = outp.tile([P, 512], F32, name="o_sb", tag="o_sb")
                         o_v = o_sb[:].rearrange("p (a b) -> p a b", a=2)
                         copy_on("s", o_v, o_ps[tp][:])
                         t8 = 4 * half + 2 * tp
-                        nc.sync.dma_start(out=o0_v[:, t8 : t8 + 2, 256:512], in_=o_v)
+                        nc.sync.dma_start(out=o0_v[:, t8 : t8 + 2, 768:1024], in_=o_v)
                 return
             half = rounds[r][0][1]
             col = P * rounds[r][0][0]
@@ -352,95 +356,112 @@ def tile_qwen2vlattention_pa_kernel(
                     copy_on(engines[t], o_sb[:], o_t[:])
                     nc.sync.dma_start(out=o0_v[:, 4 * half + t, col : col + 512], in_=o_sb[:])
 
-        keep_clock(4, 7)
-        x_transposes(0, 0, (0, 1, 2), "svs")
+        keep_clock(15, 7)
+        x_turn(0, 0, (0, 1, 2))
+        keep_clock(2, 7)
+        x_turn(0, 1, (3, 4, 5))
+        bias_ps = bias_turn(6)
+        x_turn(1, 0, (0, 1, 2))
+        keep_clock(1, 5)
+        x_turn(1, 1, (3, 4, 5))
         regroup("v", 0, 0, 0)
-        x_transposes(0, 1, (3, 4, 5), "vsv")
-        keep_clock(3, 7)
         regroup("s", 0, 0, 1)
-        quant_x(0, 0)
         quant_w(0, 0)
+        for tp in range(2):
+            for g in range(PASSES):
+                x_copy("s" if g == 0 else "v", 0, tp, g)
+        bias_copy(bias_ps)
+        for g in range(PASSES):
+            quant_x(0, g)
+        for tp in range(2):
+            for g in range(PASSES):
+                x_copy("s", 1, tp, g)
         for t in range(4):
             kv_pass(0, 0, t)
         regroup("v", 0, 1, 0)
-        regroup("s", 0, 1, 1)
-        quant_x(0, 1)
-        quant_w(0, 1)
+        regroup("v", 0, 1, 1)
         regroup("v", 0, 2, 0)
         regroup("s", 0, 2, 1)
-        quant_x(0, 2)
+        quant_x(1, 0)
+        quant_w(0, 1)
+        quant_x(1, 1)
+        quant_x(1, 2)
         quant_w(0, 2)
-        x_transposes(1, 0, (6, 7, 4), "sss")
         for t in range(4):
-            kv_pass(0, 1, t)
-        regroup("v", 1, 0, 0)
-        x_transposes(1, 1, (5, 6, 7), "sss")
-        for t in range(4):
-            kv_pass(0, 2, t)
-        bias_rows(4)
-        bias_transpose(6)
-        regroup("v", 1, 0, 1)
+            kv_pass(1, 0, t)
+        for half in range(2):
+            for t in range(4):
+                kv_pass(half, 1, t)
+        for half in range(2):
+            for t in range(4):
+                kv_pass(half, 2, t)
         for g in range(PASSES):
-            quant_x(1, g)
-        for g in range(1, PASSES):
-            regroup("v", 1, g, 0)
             regroup("s", 1, g, 1)
-        for t in range(4):
-            for g in range(PASSES):
-                kv_pass(1, g, t)
-        for t in range(4):
+        regroup("v", 1, 0, 0)
+        regroup("v", 1, 1, 0)
+        quant_w(1, 0)
+        regroup("v", 1, 2, 0)
+        quant_w(1, 1)
+        kv_add(0, 0)
+        quant_w(1, 2)
+        for t in range(1, 4):
             kv_add(0, t)
         merge_tables()
-        for g in range(PASSES):
-            quant_w(1, g)
-        table_transposes(0, 0)
-        table_transposes(1, 1)
         project(0)
         for t in range(4):
             kv_add(1, t)
-        for g in range(PASSES):
-            for part in range(2):
-                regroup("s", 2, g, part)
+        regroup("s", 2, 0, 0)
+        regroup("s", 2, 0, 1)
+        table_transposes(0, 4)
+        table_transposes(1, 5)
+        project(1)
         v_store(0)
         v_store(1)
+        for part in range(2):
+            regroup("s", 2, 1, part)
+        for part in range(2):
+            regroup("s", 2, 2, part)
+        quant_w(2, 0)
         for i in range(4):
             rope(0, i)
-        for tp in (2, 3, 0, 1):
+        for tp in (0, 1, 2, 3):
             free_rope(kv_sb, tp)
+        k_store(0)
+        for part in range(2):
+            regroup("s", 3, 0, part)
+        back(0)
+        quant_w(2, 1)
+        rope(1, 0)
+        quant_w(2, 2)
+        rope(1, 1)
+        rope(1, 2)
+        rope(1, 3)
+        for part in range(2):
+            regroup("s", 3, 1, part)
+        for part in range(2):
+            regroup("s", 3, 2, part)
         for tp in range(4):
             qb_project(tp)
-        back(0)
-        for g in range(2):
-            quant_w(2, g)
+        back(1)
         for tp in range(4):
             qb_add(tp)
+        for g in range(PASSES):
+            quant_w(3, g)
+        project(2)
         for tp in range(4):
             free_rope(qb_sb, tp)
-        quant_w(2, 2)
-        project(1)
-        for i in range(4):
-            rope(1, i)
-        for g in range(PASSES):
-            for part in range(2):
-                regroup("s", 3, g, part)
-        project(2)
-        back(1)
-        for g in range(2):
-            quant_w(3, g)
+        k_store(1)
         for i in range(4):
             rope(2, i)
-            if i == 1:
-                quant_w(3, 2)
         project(3)
         back(2)
-        k_store(0)
-        k_store(1)
         for i in range(4):
             rope(3, i)
         project(4)
+        for tp in range(3):
+            qb_store(tp)
         back(3)
-        qb_store(0)
         for i in range(4):
             rope(4, i)
+        qb_store(3)
         back(4, "svsv")
-        qb_store(1)

@@ -19,6 +19,8 @@ M = 1536
 PASSES = 3
 T8 = 8
 HALF = 512
+ACC_BANKS = (6, 7, 0, 1)
+OUT_BANKS = (2, 3, 4, 5)
 
 FLOPS = 2 * S * M * 2048
 BYTES = S * M * 2 + M * 2048 * 2 + 16 * 128 * 2 + 2 * S * 128 * 2 + S * 2048 * 4
@@ -206,7 +208,7 @@ def tile_qwen2vlattention_pa_kernel(
             )
 
         def qb_project(tp):
-            qb_acc[tp] = bank((6, 7, 4, 5)[tp], [P, 2, 256], F32)
+            qb_acc[tp] = bank(ACC_BANKS[tp], [P, 2, 256], F32)
             for tt in range(2):
                 half, t = divmod(2 * tp + tt, 4)
                 tok = slice(P * t, P * t + P)
@@ -261,7 +263,7 @@ def tile_qwen2vlattention_pa_kernel(
             for i, (head, half) in enumerate(rounds[r]):
                 j = 1 + head // 4
                 cols = slice(P * (head % 4), P * (head % 4) + P)
-                accs[(r, i)] = bank(i if r == 0 else (6, 7, 4, 5)[i], [P, HALF], F32)
+                accs[(r, i)] = bank(OUT_BANKS[i] if r == 0 else ACC_BANKS[i], [P, HALF], F32)
                 for g in range(PASSES):
                     nc.tensor.matmul_mx(
                         out=accs[(r, i)][:],
@@ -274,9 +276,9 @@ def tile_qwen2vlattention_pa_kernel(
                     )
 
         def keep_clock(n, b):
+            spare = bank(b, [P, 512], F32)
             for i in range(n):
-                spare = bank(b, [P, 512], F32)
-                nc.tensor.matmul(out=spare[:], lhsT=busy[:, 0:P], rhs=busy[:], start=True, stop=True)
+                nc.tensor.matmul(out=spare[:], lhsT=busy[:, 0:P], rhs=busy[:], start=(i == 0), stop=(i == n - 1))
 
         def bias_turn(b):
             bias_ps = [bank(b, [P, 512], F32), bank(b + 1, [P, 272], F32)]
@@ -332,7 +334,7 @@ def tile_qwen2vlattention_pa_kernel(
         def back(r, engines="ssss"):
             if r == 2:
                 for half in range(2):
-                    o_ps = [bank(2 * half + tp, [P, 2, 256], F32) for tp in range(2)]
+                    o_ps = [bank(OUT_BANKS[2 * half + tp], [P, 2, 256], F32) for tp in range(2)]
                     for hh in range(2):
                         cols = slice(P * hh, P * hh + P)
                         for tt in range(2):
@@ -348,7 +350,7 @@ def tile_qwen2vlattention_pa_kernel(
             col = P * rounds[r][0][0]
             for tp in range(2):
                 pair = (2 * tp, 2 * tp + 1)
-                o_ps = [bank(t, [P, 512], F32) for t in pair]
+                o_ps = [bank(OUT_BANKS[t], [P, 512], F32) for t in pair]
                 for hh in range(4):
                     turn([o[:, P * hh : P * hh + P] for o in o_ps], uws[(r, hh)], pair)
                 for o_t, t in zip(o_ps, pair):
@@ -356,13 +358,13 @@ def tile_qwen2vlattention_pa_kernel(
                     copy_on(engines[t], o_sb[:], o_t[:])
                     nc.sync.dma_start(out=o0_v[:, 4 * half + t, col : col + 512], in_=o_sb[:])
 
-        keep_clock(15, 7)
+        keep_clock(11, 7)
         x_turn(0, 0, (0, 1, 2))
         keep_clock(2, 7)
         x_turn(0, 1, (3, 4, 5))
         bias_ps = bias_turn(6)
         x_turn(1, 0, (0, 1, 2))
-        keep_clock(1, 5)
+        keep_clock(2, 5)
         x_turn(1, 1, (3, 4, 5))
         regroup("v", 0, 0, 0)
         regroup("s", 0, 0, 1)
@@ -407,13 +409,13 @@ def tile_qwen2vlattention_pa_kernel(
         for t in range(1, 4):
             kv_add(0, t)
         merge_tables()
-        project(0)
+        regroup("s", 2, 0, 0)
+        table_transposes(0, 0)
+        table_transposes(1, 1)
         for t in range(4):
             kv_add(1, t)
-        regroup("s", 2, 0, 0)
         regroup("s", 2, 0, 1)
-        table_transposes(0, 4)
-        table_transposes(1, 5)
+        project(0)
         project(1)
         v_store(0)
         v_store(1)
@@ -421,8 +423,9 @@ def tile_qwen2vlattention_pa_kernel(
             regroup("s", 2, 1, part)
         for part in range(2):
             regroup("s", 2, 2, part)
+        rope(0, 0)
         quant_w(2, 0)
-        for i in range(4):
+        for i in range(1, 4):
             rope(0, i)
         for tp in (0, 1, 2, 3):
             free_rope(kv_sb, tp)

@@ -9,9 +9,7 @@ U32 = mybir.dt.uint32
 U8 = mybir.dt.uint8
 FP8X4 = mybir.dt.float8_e4m3fn_x4
 ADD = mybir.AluOpType.add
-SUB = mybir.AluOpType.subtract
 MULT = mybir.AluOpType.mult
-ACT = mybir.ActivationFunctionType
 
 P = 128
 S = 1024
@@ -61,7 +59,6 @@ def tile_qwen2vlattention_pa_kernel(
         ident_b = keep.tile([P, P], BF16, name="ident_b")
         perm_f = keep.tile([P, P], F32, name="perm_f")
         ones_b = keep.tile([P, P], BF16, name="ones_b")
-        sgn = keep.tile([P, 1], F32, name="sgn")
         busy = keep.tile([P, 512], BF16, name="busy")
         warm = keep.tile([P, 1], F32, name="warm")
         b_raw = keep.tile([P, P], BF16, name="b_raw")
@@ -86,9 +83,7 @@ def tile_qwen2vlattention_pa_kernel(
         x_w = x_raw[:].bitcast(F32)
 
         nc.vector.memset(busy[:], 0.0)
-        nc.vector.memset(sgn[0:64, :], 1.0)
-        nc.vector.memset(sgn[64:128, :], -1.0)
-        nc.scalar.copy(out=warm[:], in_=sgn[:])
+        nc.scalar.copy(out=warm[:], in_=busy[:, 0:1])
         make_identity(nc, ident_f[:])
         make_identity(nc, ident_b[:])
         nc.vector.memset(row_b[:], 0.0)
@@ -235,21 +230,26 @@ def tile_qwen2vlattention_pa_kernel(
             ts = slice(4 * half, 4 * half + 4)
             nc.sync.dma_start(out=o2_v[:, ts, :], in_=kv_sb[:, ts, 256:512])
 
-        def free_rope(tile, tp):
-            ts = slice(2 * tp, 2 * tp + 2)
+        def free_rope(tile, t0, nt):
+            ts = slice(t0, t0 + nt)
             y = tile[:, ts, 0:256].rearrange("p t (h d) -> p t h d", h=2)
-            c_b = c_raw[:, ts, :].unsqueeze(2).to_broadcast([P, 2, 2, P])
-            s_b = s_raw[:, ts, :].unsqueeze(2).to_broadcast([P, 2, 2, P])
-            a = krp.tile([P, 2, 2, P], F32, name="ka", tag="ka")
-            w = krp.tile([P, 2, 2, P], F32, name="kw", tag="kw")
+            c_b = c_raw[:, ts, :].unsqueeze(2).to_broadcast([P, nt, 2, P])
+            s_b = s_raw[:, ts, :].unsqueeze(2).to_broadcast([P, nt, 2, P])
+            a = krp.tile([P, nt, 2, P], F32, name="ka", tag="ka")
+            w = krp.tile([P, nt, 2, P], F32, name="kw", tag="kw")
             nc.gpsimd.tensor_tensor(out=a[:], in0=y, in1=c_b, op=MULT)
             nc.gpsimd.tensor_tensor(out=w[:], in0=y, in1=s_b, op=MULT)
-            nc.gpsimd.tensor_tensor(out=y[:, :, :, 0:64], in0=a[:, :, :, 0:64], in1=w[:, :, :, 64:128], op=SUB)
-            nc.gpsimd.tensor_tensor(out=y[:, :, :, 64:128], in0=a[:, :, :, 64:128], in1=w[:, :, :, 0:64], op=ADD)
+            halves = "p t h (two d) -> p t h two d"
+            nc.gpsimd.tensor_tensor(
+                out=y.rearrange(halves, two=2),
+                in0=a[:].rearrange(halves, two=2),
+                in1=w[:].rearrange(halves, two=2)[:, :, :, ::-1, :],
+                op=ADD,
+            )
 
-        def qb_store(tp):
+        def qb_store(tp, queue=nc.sync):
             ts = slice(2 * tp, 2 * tp + 2)
-            nc.sync.dma_start(out=o0_v[:, ts, 512:768], in_=qb_sb[:, ts, :])
+            queue.dma_start(out=o0_v[:, ts, 512:768], in_=qb_sb[:, ts, :])
 
         def k_store(half):
             ts = slice(4 * half, 4 * half + 4)
@@ -295,7 +295,11 @@ def tile_qwen2vlattention_pa_kernel(
             for comp, lo, hi, dlo in COS_PARTS:
                 nc.scalar.copy(out=c_raw[:, :, dlo : dlo + hi - lo], in_=c_all[:, comp, :, lo:hi])
             for comp, lo, hi, dlo in SIN_PARTS:
-                nc.scalar.copy(out=s_raw[:, :, dlo : dlo + hi - lo], in_=s_all[:, comp, :, lo:hi])
+                out = s_raw[:, :, dlo : dlo + hi - lo]
+                if dlo < 64:
+                    nc.scalar.copy(out=out, in_=s_all[:, comp, :, lo:hi])
+                else:
+                    nc.scalar.mul(out, s_all[:, comp, :, lo:hi], -1.0)
 
         def table_transposes(half, b):
             tb = bank(b, [P, 2, HALF], BF16)
@@ -304,7 +308,7 @@ def tile_qwen2vlattention_pa_kernel(
             for t in range(4):
                 nc.tensor.transpose(tb[:, 1, P * t : P * t + P], s_raw[:, 4 * half + t, :], ident_b[:])
             nc.scalar.copy(out=tab_t[:, half, 0, :], in_=tb[:, 0, :])
-            nc.scalar.activation(out=tab_t[:, half, 1, :], in_=tb[:, 1, :], func=ACT.Copy, scale=sgn[:, 0:1])
+            nc.scalar.copy(out=tab_t[:, half, 1, :], in_=tb[:, 1, :])
 
         def rope(r, i):
             head, half = rounds[r][i]
@@ -423,19 +427,19 @@ def tile_qwen2vlattention_pa_kernel(
             regroup("s", 2, 1, part)
         for part in range(2):
             regroup("s", 2, 2, part)
-        rope(0, 0)
-        quant_w(2, 0)
-        for i in range(1, 4):
+        for i in range(4):
             rope(0, i)
-        for tp in (0, 1, 2, 3):
-            free_rope(kv_sb, tp)
+        free_rope(kv_sb, 0, 2)
+        free_rope(kv_sb, 2, 2)
+        free_rope(kv_sb, 4, 2)
+        free_rope(kv_sb, 6, 2)
         k_store(0)
         for part in range(2):
             regroup("s", 3, 0, part)
         back(0)
-        quant_w(2, 1)
         rope(1, 0)
-        quant_w(2, 2)
+        for g in range(PASSES):
+            quant_w(2, g)
         rope(1, 1)
         rope(1, 2)
         rope(1, 3)
@@ -451,8 +455,10 @@ def tile_qwen2vlattention_pa_kernel(
         for g in range(PASSES):
             quant_w(3, g)
         project(2)
-        for tp in range(4):
-            free_rope(qb_sb, tp)
+        free_rope(qb_sb, 0, 2)
+        free_rope(qb_sb, 2, 2)
+        free_rope(qb_sb, 4, 2)
+        free_rope(qb_sb, 6, 2)
         k_store(1)
         for i in range(4):
             rope(2, i)
@@ -461,10 +467,11 @@ def tile_qwen2vlattention_pa_kernel(
         for i in range(4):
             rope(3, i)
         project(4)
-        for tp in range(3):
+        for tp in range(2):
             qb_store(tp)
         back(3)
+        qb_store(2)
         for i in range(4):
             rope(4, i)
-        qb_store(3)
+        qb_store(3, nc.gpsimd)
         back(4, "svsv")

@@ -9,7 +9,9 @@ U32 = mybir.dt.uint32
 U8 = mybir.dt.uint8
 FP8X4 = mybir.dt.float8_e4m3fn_x4
 ADD = mybir.AluOpType.add
+SUB = mybir.AluOpType.subtract
 MULT = mybir.AluOpType.mult
+ACT = mybir.ActivationFunctionType
 
 P = 128
 S = 1024
@@ -44,7 +46,7 @@ def tile_qwen2vlattention_pa_kernel(
     with ExitStack() as ctx:
         keep = ctx.enter_context(tc.tile_pool(name="keep", bufs=1))
         xgp = ctx.enter_context(tc.tile_pool(name="xgp", bufs=4))
-        wrp = ctx.enter_context(tc.tile_pool(name="wrp", bufs=8))
+        wrp = ctx.enter_context(tc.tile_pool(name="wrp", bufs=6))
         wgp = ctx.enter_context(tc.tile_pool(name="wgp", bufs=4))
         uwp = ctx.enter_context(tc.tile_pool(name="uwp", bufs=2))
         krp = ctx.enter_context(tc.tile_pool(name="krp", bufs=2))
@@ -59,6 +61,7 @@ def tile_qwen2vlattention_pa_kernel(
         ident_b = keep.tile([P, P], BF16, name="ident_b")
         perm_f = keep.tile([P, P], F32, name="perm_f")
         ones_b = keep.tile([P, P], BF16, name="ones_b")
+        sgn = keep.tile([P, 1], F32, name="sgn")
         busy = keep.tile([P, 512], BF16, name="busy")
         warm = keep.tile([P, 1], F32, name="warm")
         b_raw = keep.tile([P, P], BF16, name="b_raw")
@@ -83,7 +86,9 @@ def tile_qwen2vlattention_pa_kernel(
         x_w = x_raw[:].bitcast(F32)
 
         nc.vector.memset(busy[:], 0.0)
-        nc.scalar.copy(out=warm[:], in_=busy[:, 0:1])
+        nc.vector.memset(sgn[0:64, :], 1.0)
+        nc.vector.memset(sgn[64:128, :], -1.0)
+        nc.scalar.copy(out=warm[:], in_=sgn[:])
         make_identity(nc, ident_f[:])
         make_identity(nc, ident_b[:])
         nc.vector.memset(row_b[:], 0.0)
@@ -239,13 +244,8 @@ def tile_qwen2vlattention_pa_kernel(
             w = krp.tile([P, nt, 2, P], F32, name="kw", tag="kw")
             nc.gpsimd.tensor_tensor(out=a[:], in0=y, in1=c_b, op=MULT)
             nc.gpsimd.tensor_tensor(out=w[:], in0=y, in1=s_b, op=MULT)
-            halves = "p t h (two d) -> p t h two d"
-            nc.gpsimd.tensor_tensor(
-                out=y.rearrange(halves, two=2),
-                in0=a[:].rearrange(halves, two=2),
-                in1=w[:].rearrange(halves, two=2)[:, :, :, ::-1, :],
-                op=ADD,
-            )
+            nc.gpsimd.tensor_tensor(out=y[:, :, :, 0:64], in0=a[:, :, :, 0:64], in1=w[:, :, :, 64:128], op=SUB)
+            nc.gpsimd.tensor_tensor(out=y[:, :, :, 64:128], in0=a[:, :, :, 64:128], in1=w[:, :, :, 0:64], op=ADD)
 
         def qb_store(tp, queue=nc.sync):
             ts = slice(2 * tp, 2 * tp + 2)
@@ -295,11 +295,7 @@ def tile_qwen2vlattention_pa_kernel(
             for comp, lo, hi, dlo in COS_PARTS:
                 nc.scalar.copy(out=c_raw[:, :, dlo : dlo + hi - lo], in_=c_all[:, comp, :, lo:hi])
             for comp, lo, hi, dlo in SIN_PARTS:
-                out = s_raw[:, :, dlo : dlo + hi - lo]
-                if dlo < 64:
-                    nc.scalar.copy(out=out, in_=s_all[:, comp, :, lo:hi])
-                else:
-                    nc.scalar.mul(out, s_all[:, comp, :, lo:hi], -1.0)
+                nc.scalar.copy(out=s_raw[:, :, dlo : dlo + hi - lo], in_=s_all[:, comp, :, lo:hi])
 
         def table_transposes(half, b):
             tb = bank(b, [P, 2, HALF], BF16)
@@ -308,7 +304,7 @@ def tile_qwen2vlattention_pa_kernel(
             for t in range(4):
                 nc.tensor.transpose(tb[:, 1, P * t : P * t + P], s_raw[:, 4 * half + t, :], ident_b[:])
             nc.scalar.copy(out=tab_t[:, half, 0, :], in_=tb[:, 0, :])
-            nc.scalar.copy(out=tab_t[:, half, 1, :], in_=tb[:, 1, :])
+            nc.scalar.activation(out=tab_t[:, half, 1, :], in_=tb[:, 1, :], func=ACT.Copy, scale=sgn[:, 0:1])
 
         def rope(r, i):
             head, half = rounds[r][i]
@@ -379,17 +375,18 @@ def tile_qwen2vlattention_pa_kernel(
         bias_copy(bias_ps)
         for g in range(PASSES):
             quant_x(0, g)
-        for tp in range(2):
-            for g in range(PASSES):
-                x_copy("s", 1, tp, g)
+        for g in range(PASSES):
+            x_copy("s", 1, 0, g)
+        regroup("s", 0, 1, 1)
+        for g in range(PASSES):
+            x_copy("s", 1, 1, g)
         for t in range(4):
             kv_pass(0, 0, t)
         regroup("v", 0, 1, 0)
-        regroup("v", 0, 1, 1)
         regroup("v", 0, 2, 0)
         regroup("s", 0, 2, 1)
-        quant_x(1, 0)
         quant_w(0, 1)
+        quant_x(1, 0)
         quant_x(1, 1)
         quant_x(1, 2)
         quant_w(0, 2)
@@ -403,14 +400,15 @@ def tile_qwen2vlattention_pa_kernel(
                 kv_pass(half, 2, t)
         for g in range(PASSES):
             regroup("s", 1, g, 1)
+        regroup("s", 1, 2, 0)
         regroup("v", 1, 0, 0)
         regroup("v", 1, 1, 0)
         quant_w(1, 0)
-        regroup("v", 1, 2, 0)
         quant_w(1, 1)
         kv_add(0, 0)
+        kv_add(0, 1)
         quant_w(1, 2)
-        for t in range(1, 4):
+        for t in range(2, 4):
             kv_add(0, t)
         merge_tables()
         regroup("s", 2, 0, 0)
@@ -455,8 +453,7 @@ def tile_qwen2vlattention_pa_kernel(
         for g in range(PASSES):
             quant_w(3, g)
         project(2)
-        free_rope(qb_sb, 0, 2)
-        free_rope(qb_sb, 2, 2)
+        free_rope(qb_sb, 0, 4)
         free_rope(qb_sb, 4, 2)
         free_rope(qb_sb, 6, 2)
         k_store(1)

@@ -50,7 +50,7 @@ def tile_qwen2vlattention_pa_kernel(
         wgp = ctx.enter_context(tc.tile_pool(name="wgp", bufs=4))
         uwp = ctx.enter_context(tc.tile_pool(name="uwp", bufs=2))
         krp = ctx.enter_context(tc.tile_pool(name="krp", bufs=2))
-        outp = ctx.enter_context(tc.tile_pool(name="outp", bufs=7))
+        outp = ctx.enter_context(tc.tile_pool(name="outp", bufs=6))
         psum = ctx.enter_context(tc.psum_pool(name="psum", bufs=1))
         ctx.enter_context(tc.manual_schedule())
 
@@ -75,10 +75,10 @@ def tile_qwen2vlattention_pa_kernel(
         s_raw = keep.tile([P, T8, P], BF16, name="s_raw")
         tab_t = keep.tile([P, 2, 2, HALF], BF16, name="tab_t")
         x_raw = keep.tile([P, T8 * M], BF16, name="x_raw")
-        xq = keep.tile([P, 2, PASSES, HALF], U32, name="xq", align_bytes=64)
-        xs = keep.tile([P, 2, PASSES, HALF], U8, name="xs", align_bytes=64)
-        wq = [keep.tile([P, PASSES, 512], U32, name="wq%d" % j, align_bytes=64) for j in range(4)]
-        ws = [keep.tile([P, PASSES, 512], U8, name="ws%d" % j, align_bytes=64) for j in range(4)]
+        xq = keep.tile([P, 2, PASSES, HALF], U32, name="xq", align_bytes=256)
+        xs = keep.tile([P, 2, PASSES, HALF], U8, name="xs", align_bytes=256)
+        wq = [keep.tile([P, PASSES, 512], U32, name="wq%d" % j, align_bytes=256) for j in range(4)]
+        ws = [keep.tile([P, PASSES, 512], U8, name="ws%d" % j, align_bytes=256) for j in range(4)]
         w_raw = [
             [wrp.tile([P, 2, 4, 256] if j == 0 else [P, 1, 4, 512], BF16, name="wraw", tag="wraw") for g in range(PASSES)]
             for j in range(4)

@@ -97,8 +97,8 @@ def tile_qwen2vlattention_pa_kernel(
         nc.vector.tensor_copy(out=perm_f[:, 0:64], in_=ident_f[:, 64:128])
         nc.vector.tensor_copy(out=perm_f[:, 64:128], in_=ident_f[:, 0:64])
 
-        def load_x(half):
-            for tp in range(2):
+        def load_x(half, pairs=range(2)):
+            for tp in pairs:
                 t8 = 4 * half + 2 * tp
                 nc.sync.dma_start(
                     out=x_raw[:, t8 * M : (t8 + 2) * M],
@@ -126,8 +126,9 @@ def tile_qwen2vlattention_pa_kernel(
         nc.scalar.dma_start(out=row_b[0:1, 256:512], in_=bv.rearrange("(o h) d -> o (h d)", o=1))
         nc.scalar.dma_start(out=row_b[0:1, 512:768], in_=bq[4:6, :].rearrange("(o h) d -> o (h d)", o=1))
         nc.scalar.dma_start(out=b_raw[0:12, :], in_=bq)
+        load_x(0, (0,))
         load_w(0, (0,))
-        load_x(0)
+        load_x(0, (1,))
         load_x(1)
         load_w(0, (1, 2))
         load_w(1)
@@ -358,13 +359,13 @@ def tile_qwen2vlattention_pa_kernel(
                     copy_on(engines[t], o_sb[:], o_t[:])
                     nc.sync.dma_start(out=o0_v[:, 4 * half + t, col : col + 512], in_=o_sb[:])
 
-        keep_clock(11, 7)
+        keep_clock(7, 7)
         x_turn(0, 0, (0, 1, 2))
         keep_clock(2, 7)
         x_turn(0, 1, (3, 4, 5))
         bias_ps = bias_turn(6)
         x_turn(1, 0, (0, 1, 2))
-        keep_clock(2, 5)
+        keep_clock(1, 5)
         x_turn(1, 1, (3, 4, 5))
         regroup("v", 0, 0, 0)
         regroup("s", 0, 0, 1)
@@ -443,15 +444,16 @@ def tile_qwen2vlattention_pa_kernel(
         rope(1, 3)
         for part in range(2):
             regroup("s", 3, 1, part)
-        for part in range(2):
-            regroup("s", 3, 2, part)
+        regroup("s", 3, 2, 0)
         for tp in range(4):
             qb_project(tp)
         back(1)
         for tp in range(4):
             qb_add(tp)
-        for g in range(PASSES):
-            quant_w(3, g)
+        quant_w(3, 0)
+        regroup("v", 3, 2, 1)
+        quant_w(3, 1)
+        quant_w(3, 2)
         project(2)
         free_rope(qb_sb, 0, 4)
         free_rope(qb_sb, 4, 2)

@@ -349,8 +349,7 @@ def tile_qwen2vlattention_pa_kernel(
                 return
             half = rounds[r][0][1]
             col = P * rounds[r][0][0]
-            for tp in range(2):
-                pair = (2 * tp, 2 * tp + 1)
+            for pair in ((0,), (1,), (2,), (3,)):
                 o_ps = [bank(OUT_BANKS[t], [P, 512], F32) for t in pair]
                 for hh in range(4):
                     turn([o[:, P * hh : P * hh + P] for o in o_ps], uws[(r, hh)], pair)
@@ -378,7 +377,7 @@ def tile_qwen2vlattention_pa_kernel(
             quant_x(0, g)
         for g in range(PASSES):
             x_copy("s", 1, 0, g)
-        regroup("s", 0, 1, 1)
+        regroup("g", 0, 1, 1)
         for g in range(PASSES):
             x_copy("s", 1, 1, g)
         for t in range(4):
@@ -469,8 +468,8 @@ def tile_qwen2vlattention_pa_kernel(
         for tp in range(2):
             qb_store(tp)
         back(3)
-        qb_store(2)
         for i in range(4):
             rope(4, i)
+        qb_store(2, nc.gpsimd)
         qb_store(3, nc.gpsimd)
         back(4, "svsv")

@@ -377,7 +377,7 @@ def tile_qwen2vlattention_pa_kernel(
             quant_x(0, g)
         for g in range(PASSES):
             x_copy("s", 1, 0, g)
-        regroup("g", 0, 1, 1)
+        regroup("s", 0, 1, 1)
         for g in range(PASSES):
             x_copy("s", 1, 1, g)
         for t in range(4):
@@ -468,8 +468,8 @@ def tile_qwen2vlattention_pa_kernel(
         for tp in range(2):
             qb_store(tp)
         back(3)
+        qb_store(2, nc.scalar)
         for i in range(4):
             rope(4, i)
-        qb_store(2, nc.gpsimd)
-        qb_store(3, nc.gpsimd)
         back(4, "svsv")
+        qb_store(3, nc.scalar)

from contextlib import ExitStack

import concourse.mybir as mybir
from concourse.masks import make_identity

F32 = mybir.dt.float32
BF16 = mybir.dt.bfloat16
U32 = mybir.dt.uint32
U8 = mybir.dt.uint8
FP8X4 = mybir.dt.float8_e4m3fn_x4
ADD = mybir.AluOpType.add
SUB = mybir.AluOpType.subtract
MULT = mybir.AluOpType.mult
ACT = mybir.ActivationFunctionType

P = 128
S = 1024
M = 1536
PASSES = 3
T8 = 8
HALF = 512
ACC_BANKS = (6, 7, 0, 1)
OUT_BANKS = (2, 3, 4, 5)

FLOPS = 2 * S * M * 2048
BYTES = S * M * 2 + M * 2048 * 2 + 16 * 128 * 2 + 2 * S * 128 * 2 + S * 2048 * 4

COS_PARTS = ((0, 0, 32, 0), (1, 32, 80, 32), (2, 80, 128, 80))
SIN_PARTS = ((1, 64, 80, 0), (2, 80, 128, 16), (0, 0, 32, 64), (1, 32, 64, 96))


def tile_qwen2vlattention_pa_kernel(
    tc, hidden_states, cos, sin, Wq, bq, Wk, bk, Wv, bv, out_0, out_1, out_2
):
    nc = tc.nc
    x_v = hidden_states.rearrange("b s m -> (b s) m").rearrange("(p t) m -> p t m", t=T8)
    cos_v = cos.rearrange("c b s d -> c (b s) d")
    sin_v = sin.rearrange("c b s d -> c (b s) d")
    wq_v = Wq.rearrange("m h d -> m (h d)")
    wk_v = Wk.rearrange("m h d -> m (h d)")
    wv_v = Wv.rearrange("m h d -> m (h d)")
    o0_v = out_0.rearrange("b s h d -> (b s) (h d)").rearrange("(p t) n -> p t n", t=T8)
    o1_v = out_1.rearrange("b s h d -> (b s) (h d)").rearrange("(p t) n -> p t n", t=T8)
    o2_v = out_2.rearrange("b s h d -> (b s) (h d)").rearrange("(p t) n -> p t n", t=T8)

    with ExitStack() as ctx:
        keep = ctx.enter_context(tc.tile_pool(name="keep", bufs=1))
        xgp = ctx.enter_context(tc.tile_pool(name="xgp", bufs=4))
        wrp = ctx.enter_context(tc.tile_pool(name="wrp", bufs=6))
        wgp = ctx.enter_context(tc.tile_pool(name="wgp", bufs=4))
        uwp = ctx.enter_context(tc.tile_pool(name="uwp", bufs=2))
        krp = ctx.enter_context(tc.tile_pool(name="krp", bufs=2))
        outp = ctx.enter_context(tc.tile_pool(name="outp", bufs=6))
        psum = ctx.enter_context(tc.psum_pool(name="psum", bufs=1))
        ctx.enter_context(tc.manual_schedule())

        def bank(i, shape, dtype):
            return psum.tile(shape, dtype, name="bank%d" % i, tag="bank%d" % i)

        ident_f = keep.tile([P, P], F32, name="ident_f")
        ident_b = keep.tile([P, P], BF16, name="ident_b")
        perm_f = keep.tile([P, P], F32, name="perm_f")
        ones_b = keep.tile([P, P], BF16, name="ones_b")
        sgn = keep.tile([P, 1], F32, name="sgn")
        busy = keep.tile([P, 512], BF16, name="busy")
        warm = keep.tile([P, 1], F32, name="warm")
        b_raw = keep.tile([P, P], BF16, name="b_raw")
        row_b = keep.tile([P, 768], BF16, name="row_b")
        free_b = keep.tile([P, 784], F32, name="free_b")
        qb_sb = keep.tile([P, T8, 256], F32, name="qb_sb")
        kv_sb = keep.tile([P, T8, 512], F32, name="kv_sb")
        c_all = keep.tile([P, 3, T8, P], BF16, name="c_all")
        s_all = keep.tile([P, 3, T8, P], BF16, name="s_all")
        c_raw = keep.tile([P, T8, P], BF16, name="c_raw")
        s_raw = keep.tile([P, T8, P], BF16, name="s_raw")
        tab_t = keep.tile([P, 2, 2, HALF], BF16, name="tab_t")
        x_raw = keep.tile([P, T8 * M], BF16, name="x_raw")
        xq = keep.tile([P, 2, PASSES, HALF], U32, name="xq", align_bytes=256)
        xs = keep.tile([P, 2, PASSES, HALF], U8, name="xs", align_bytes=256)
        wq = [keep.tile([P, PASSES, 512], U32, name="wq%d" % j, align_bytes=256) for j in range(4)]
        ws = [keep.tile([P, PASSES, 512], U8, name="ws%d" % j, align_bytes=256) for j in range(4)]
        w_raw = [
            [wrp.tile([P, 2, 4, 256] if j == 0 else [P, 1, 4, 512], BF16, name="wraw", tag="wraw") for g in range(PASSES)]
            for j in range(4)
        ]
        x_w = x_raw[:].bitcast(F32)

        nc.vector.memset(busy[:], 0.0)
        nc.vector.memset(sgn[0:64, :], 1.0)
        nc.vector.memset(sgn[64:128, :], -1.0)
        nc.scalar.copy(out=warm[:], in_=sgn[:])
        make_identity(nc, ident_f[:])
        make_identity(nc, ident_b[:])
        nc.vector.memset(row_b[:], 0.0)
        nc.vector.memset(b_raw[:], 0.0)
        nc.vector.memset(ones_b[:], 1.0)
        nc.vector.tensor_copy(out=perm_f[:, 0:64], in_=ident_f[:, 64:128])
        nc.vector.tensor_copy(out=perm_f[:, 64:128], in_=ident_f[:, 0:64])

        def load_x(half, pairs=range(2)):
            for tp in pairs:
                t8 = 4 * half + 2 * tp
                nc.sync.dma_start(
                    out=x_raw[:, t8 * M : (t8 + 2) * M],
                    in_=x_v[:, t8 : t8 + 2, :].rearrange("p t m -> p (t m)"),
                )

        def load_w(j, passes=range(PASSES)):
            for g in passes:
                rows = slice(512 * g, 512 * g + 512)
                if j == 0:
                    sources = (wk_v[rows, :], wv_v[rows, :])
                else:
                    sources = (wq_v[rows, 512 * (j - 1) : 512 * j],)
                for blk, src in enumerate(sources):
                    nc.sync.dma_start(
                        out=w_raw[j][g][:, blk],
                        in_=src.rearrange("(q e) n -> q e n", e=4),
                    )

        def load_tables():
            for table, view in ((c_all, cos_v), (s_all, sin_v)):
                nc.sync.dma_start(out=table[:], in_=view.rearrange("c (p t) d -> p c t d", t=T8))

        nc.scalar.dma_start(out=row_b[0:1, 0:256], in_=bk.rearrange("(o h) d -> o (h d)", o=1))
        nc.scalar.dma_start(out=row_b[0:1, 256:512], in_=bv.rearrange("(o h) d -> o (h d)", o=1))
        nc.scalar.dma_start(out=row_b[0:1, 512:768], in_=bq[4:6, :].rearrange("(o h) d -> o (h d)", o=1))
        nc.scalar.dma_start(out=b_raw[0:12, :], in_=bq)
        load_x(0, (0,))
        load_w(0, (0,))
        load_x(0, (1,))
        load_x(1)
        load_w(0, (1, 2))
        load_w(1)
        load_tables()
        load_w(2)
        load_w(3)

        xg = {}
        wg = {}
        accs = {}
        uws = {}

        def copy_on(engine, out, in_):
            if engine == "v":
                nc.vector.tensor_copy(out=out, in_=in_)
            elif engine == "s":
                nc.scalar.copy(out=out, in_=in_)
            else:
                nc.gpsimd.tensor_scalar(out=out, in0=in_, scalar1=1.0, scalar2=0.0, op0=MULT, op1=ADD)

        x_ps = {}

        def x_turn(half, tp, banks):
            for g in range(PASSES):
                xt = bank(banks[g], [P, 2, 2, P], F32)
                x_ps[(half, tp, g)] = xt
                for tt in range(2):
                    for u in range(2):
                        col = (4 * half + 2 * tp + tt) * (M // 2) + 256 * g
                        nc.tensor.transpose(xt[:, tt, u, :], x_w[:, col + u : col + 256 : 2], ident_f[:])

        def x_copy(engine, half, tp, g):
            if (half, g) not in xg:
                xg[(half, g)] = xgp.tile([P, 2048], BF16, name="xg", tag="xg", align_bytes=64)
            words = xg[(half, g)][:].bitcast(F32).rearrange("p (tt s u) -> p tt s u", tt=4, u=2)
            copy_on(engine, words[:, 2 * tp : 2 * tp + 2], x_ps[(half, tp, g)][:].rearrange("p tt u s -> p tt s u"))

        def quant_x(half, g):
            nc.vector.quantize_mx(
                out=xq[:, half, g, :].bitcast(FP8X4), scales=xs[:, half, g, :], in_=xg[(half, g)][:]
            )

        def regroup(engine, j, g, part):
            if (j, g) not in wg:
                wg[(j, g)] = wgp.tile([P, 2048], BF16, name="wg", tag="wg", align_bytes=64)
            dst = wg[(j, g)][:, 1024 * part : 1024 * part + 1024].rearrange("p (c i t) -> p c t i", i=4, t=4)
            if j == 0:
                src = w_raw[j][g][:, part]
            else:
                src = w_raw[j][g][:, 0, :, 256 * part : 256 * part + 256]
            copy_on(engine, dst, src.rearrange("p t (c i) -> p c t i", i=4))

        def quant_w(j, g):
            nc.vector.quantize_mx(
                out=wq[j][:, g, :].bitcast(FP8X4), scales=ws[j][:, g, :], in_=wg[(j, g)][:]
            )

        kv_acc = {}
        qb_acc = {}

        def kv_pass(half, g, t):
            if g == 0:
                kv_acc[(half, t)] = bank(4 * half + t, [P, 512], F32)
            tok = slice(P * t, P * t + P)
            nc.tensor.matmul_mx(
                out=kv_acc[(half, t)][:],
                lhsT=xq[:, half, g, tok].bitcast(FP8X4),
                lhsT_scale=xs[:, half, g, tok],
                rhs=wq[0][:, g, :].bitcast(FP8X4),
                rhs_scale=ws[0][:, g, :],
                start=(g == 0),
                stop=(g == PASSES - 1),
            )

        def kv_add(half, t):
            nc.vector.tensor_tensor(
                out=kv_sb[:, 4 * half + t, :], in0=kv_acc[(half, t)][:], in1=free_b[:, 0:512], op=ADD
            )

        def qb_project(tp):
            qb_acc[tp] = bank(ACC_BANKS[tp], [P, 2, 256], F32)
            for tt in range(2):
                half, t = divmod(2 * tp + tt, 4)
                tok = slice(P * t, P * t + P)
                for g in range(PASSES):
                    nc.tensor.matmul_mx(
                        out=qb_acc[tp][:, tt, :],
                        lhsT=xq[:, half, g, tok].bitcast(FP8X4),
                        lhsT_scale=xs[:, half, g, tok],
                        rhs=wq[2][:, g, 0:256].bitcast(FP8X4),
                        rhs_scale=ws[2][:, g, 0:256],
                        start=(g == 0),
                        stop=(g == PASSES - 1),
                    )

        def qb_add(tp):
            nc.vector.tensor_tensor(
                out=qb_sb[:, 2 * tp : 2 * tp + 2, :],
                in0=qb_acc[tp][:],
                in1=free_b[:, 512:768].unsqueeze(1).to_broadcast([P, 2, 256]),
                op=ADD,
            )

        def v_store(half):
            ts = slice(4 * half, 4 * half + 4)
            nc.sync.dma_start(out=o2_v[:, ts, :], in_=kv_sb[:, ts, 256:512])

        def free_rope(tile, t0, nt):
            ts = slice(t0, t0 + nt)
            y = tile[:, ts, 0:256].rearrange("p t (h d) -> p t h d", h=2)
            c_b = c_raw[:, ts, :].unsqueeze(2).to_broadcast([P, nt, 2, P])
            s_b = s_raw[:, ts, :].unsqueeze(2).to_broadcast([P, nt, 2, P])
            a = krp.tile([P, nt, 2, P], F32, name="ka", tag="ka")
            w = krp.tile([P, nt, 2, P], F32, name="kw", tag="kw")
            nc.gpsimd.tensor_tensor(out=a[:], in0=y, in1=c_b, op=MULT)
            nc.gpsimd.tensor_tensor(out=w[:], in0=y, in1=s_b, op=MULT)
            nc.gpsimd.tensor_tensor(out=y[:, :, :, 0:64], in0=a[:, :, :, 0:64], in1=w[:, :, :, 64:128], op=SUB)
            nc.gpsimd.tensor_tensor(out=y[:, :, :, 64:128], in0=a[:, :, :, 64:128], in1=w[:, :, :, 0:64], op=ADD)

        def qb_store(tp, queue=nc.sync):
            ts = slice(2 * tp, 2 * tp + 2)
            queue.dma_start(out=o0_v[:, ts, 512:768], in_=qb_sb[:, ts, :])

        def k_store(half):
            ts = slice(4 * half, 4 * half + 4)
            nc.sync.dma_start(out=o1_v[:, ts, :], in_=kv_sb[:, ts, 0:256])

        rounds = [tuple((hh, half) for hh in range(4)) for half in range(2)]
        rounds.append(((6, 0), (7, 0), (6, 1), (7, 1)))
        rounds += [tuple((8 + hh, half) for hh in range(4)) for half in range(2)]

        def project(r):
            for i, (head, half) in enumerate(rounds[r]):
                j = 1 + head // 4
                cols = slice(P * (head % 4), P * (head % 4) + P)
                accs[(r, i)] = bank(OUT_BANKS[i] if r == 0 else ACC_BANKS[i], [P, HALF], F32)
                for g in range(PASSES):
                    nc.tensor.matmul_mx(
                        out=accs[(r, i)][:],
                        lhsT=wq[j][:, g, cols].bitcast(FP8X4),
                        lhsT_scale=ws[j][:, g, cols],
                        rhs=xq[:, half, g, :].bitcast(FP8X4),
                        rhs_scale=xs[:, half, g, :],
                        start=(g == 0),
                        stop=(g == PASSES - 1),
                    )

        def keep_clock(n, b):
            spare = bank(b, [P, 512], F32)
            for i in range(n):
                nc.tensor.matmul(out=spare[:], lhsT=busy[:, 0:P], rhs=busy[:], start=(i == 0), stop=(i == n - 1))

        def bias_turn(b):
            bias_ps = [bank(b, [P, 512], F32), bank(b + 1, [P, 272], F32)]
            nc.tensor.matmul(out=bias_ps[0][:], lhsT=ones_b[:], rhs=row_b[:, 0:512], start=True, stop=True)
            nc.tensor.matmul(out=bias_ps[1][:, 0:256], lhsT=ones_b[:], rhs=row_b[:, 512:768], start=True, stop=True)
            nc.tensor.matmul(out=bias_ps[1][:, 256:272], lhsT=b_raw[:], rhs=ident_b[:, 0:16], start=True, stop=True)
            return bias_ps

        def bias_copy(bias_ps):
            nc.scalar.copy(out=free_b[:, 0:512], in_=bias_ps[0][:])
            nc.scalar.copy(out=free_b[:, 512:784], in_=bias_ps[1][:])

        def merge_tables():
            for comp, lo, hi, dlo in COS_PARTS:
                nc.scalar.copy(out=c_raw[:, :, dlo : dlo + hi - lo], in_=c_all[:, comp, :, lo:hi])
            for comp, lo, hi, dlo in SIN_PARTS:
                nc.scalar.copy(out=s_raw[:, :, dlo : dlo + hi - lo], in_=s_all[:, comp, :, lo:hi])

        def table_transposes(half, b):
            tb = bank(b, [P, 2, HALF], BF16)
            for t in range(4):
                nc.tensor.transpose(tb[:, 0, P * t : P * t + P], c_raw[:, 4 * half + t, :], ident_b[:])
            for t in range(4):
                nc.tensor.transpose(tb[:, 1, P * t : P * t + P], s_raw[:, 4 * half + t, :], ident_b[:])
            nc.scalar.copy(out=tab_t[:, half, 0, :], in_=tb[:, 0, :])
            nc.scalar.activation(out=tab_t[:, half, 1, :], in_=tb[:, 1, :], func=ACT.Copy, scale=sgn[:, 0:1])

        def rope(r, i):
            head, half = rounds[r][i]
            uw = uwp.tile([P, 2, HALF], F32, name="uw%d" % i, tag="uw%d" % i)
            uws[(r, i)] = uw
            nc.vector.scalar_tensor_tensor(
                out=uw[:],
                in0=accs[(r, i)][:].unsqueeze(1).to_broadcast([P, 2, HALF]),
                scalar=free_b[:, 768 + head : 769 + head],
                in1=tab_t[:, half],
                op0=ADD,
                op1=MULT,
            )

        def turn(outs, uw, ts):
            for o, t in zip(outs, ts):
                nc.tensor.matmul(
                    out=o, lhsT=uw[:, 0, P * t : P * t + P], rhs=ident_f[:],
                    is_transpose=True, start=True, stop=False,
                )
            for o, t in zip(outs, ts):
                nc.tensor.matmul(
                    out=o, lhsT=uw[:, 1, P * t : P * t + P], rhs=perm_f[:],
                    is_transpose=True, start=False, stop=True,
                )

        def back(r, engines="ssss"):
            if r == 2:
                for half in range(2):
                    o_ps = [bank(OUT_BANKS[2 * half + tp], [P, 2, 256], F32) for tp in range(2)]
                    for hh in range(2):
                        cols = slice(P * hh, P * hh + P)
                        for tt in range(2):
                            turn([o[:, tt, cols] for o in o_ps], uws[(2, 2 * half + hh)], (tt, 2 + tt))
                    for tp in range(2):
                        o_sb = outp.tile([P, 512], F32, name="o_sb", tag="o_sb")
                        o_v = o_sb[:].rearrange("p (a b) -> p a b", a=2)
                        copy_on("s", o_v, o_ps[tp][:])
                        t8 = 4 * half + 2 * tp
                        nc.sync.dma_start(out=o0_v[:, t8 : t8 + 2, 768:1024], in_=o_v)
                return
            half = rounds[r][0][1]
            col = P * rounds[r][0][0]
            for pair in ((0,), (1,), (2,), (3,)):
                o_ps = [bank(OUT_BANKS[t], [P, 512], F32) for t in pair]
                for hh in range(4):
                    turn([o[:, P * hh : P * hh + P] for o in o_ps], uws[(r, hh)], pair)
                for o_t, t in zip(o_ps, pair):
                    o_sb = outp.tile([P, 512], F32, name="o_sb", tag="o_sb")
                    copy_on(engines[t], o_sb[:], o_t[:])
                    nc.sync.dma_start(out=o0_v[:, 4 * half + t, col : col + 512], in_=o_sb[:])

        keep_clock(7, 7)
        x_turn(0, 0, (0, 1, 2))
        keep_clock(2, 7)
        x_turn(0, 1, (3, 4, 5))
        bias_ps = bias_turn(6)
        x_turn(1, 0, (0, 1, 2))
        keep_clock(1, 5)
        x_turn(1, 1, (3, 4, 5))
        regroup("v", 0, 0, 0)
        regroup("s", 0, 0, 1)
        quant_w(0, 0)
        for tp in range(2):
            for g in range(PASSES):
                x_copy("s" if g == 0 else "v", 0, tp, g)
        bias_copy(bias_ps)
        for g in range(PASSES):
            quant_x(0, g)
        for g in range(PASSES):
            x_copy("s", 1, 0, g)
        regroup("s", 0, 1, 1)
        for g in range(PASSES):
            x_copy("s", 1, 1, g)
        for t in range(4):
            kv_pass(0, 0, t)
        regroup("v", 0, 1, 0)
        regroup("v", 0, 2, 0)
        regroup("s", 0, 2, 1)
        quant_w(0, 1)
        quant_x(1, 0)
        quant_x(1, 1)
        quant_x(1, 2)
        quant_w(0, 2)
        for t in range(4):
            kv_pass(1, 0, t)
        for half in range(2):
            for t in range(4):
                kv_pass(half, 1, t)
        for half in range(2):
            for t in range(4):
                kv_pass(half, 2, t)
        for g in range(PASSES):
            regroup("s", 1, g, 1)
        regroup("s", 1, 2, 0)
        regroup("v", 1, 0, 0)
        regroup("v", 1, 1, 0)
        quant_w(1, 0)
        quant_w(1, 1)
        kv_add(0, 0)
        kv_add(0, 1)
        quant_w(1, 2)
        for t in range(2, 4):
            kv_add(0, t)
        merge_tables()
        regroup("s", 2, 0, 0)
        table_transposes(0, 0)
        table_transposes(1, 1)
        for t in range(4):
            kv_add(1, t)
        regroup("s", 2, 0, 1)
        project(0)
        project(1)
        v_store(0)
        v_store(1)
        for part in range(2):
            regroup("s", 2, 1, part)
        for part in range(2):
            regroup("s", 2, 2, part)
        for i in range(4):
            rope(0, i)
        free_rope(kv_sb, 0, 2)
        free_rope(kv_sb, 2, 2)
        free_rope(kv_sb, 4, 2)
        free_rope(kv_sb, 6, 2)
        k_store(0)
        for part in range(2):
            regroup("s", 3, 0, part)
        back(0)
        rope(1, 0)
        for g in range(PASSES):
            quant_w(2, g)
        rope(1, 1)
        rope(1, 2)
        rope(1, 3)
        for part in range(2):
            regroup("s", 3, 1, part)
        regroup("s", 3, 2, 0)
        for tp in range(4):
            qb_project(tp)
        back(1)
        for tp in range(4):
            qb_add(tp)
        quant_w(3, 0)
        regroup("v", 3, 2, 1)
        quant_w(3, 1)
        quant_w(3, 2)
        project(2)
        free_rope(qb_sb, 0, 4)
        free_rope(qb_sb, 4, 2)
        free_rope(qb_sb, 6, 2)
        k_store(1)
        for i in range(4):
            rope(2, i)
        project(3)
        back(2)
        for i in range(4):
            rope(3, i)
        project(4)
        for tp in range(2):
            qb_store(tp)
        back(3)
        qb_store(2, nc.scalar)
        for i in range(4):
            rope(4, i)
        back(4, "svsv")
        qb_store(3, nc.scalar)
